import numpy as np
import ml_dtypes


def mxq(x, axis, fmt="e4m3"):
    dtype, down = {"e4m3": (ml_dtypes.float8_e4m3fn, 7), "e5m2": (ml_dtypes.float8_e5m2, 14)}[fmt]
    v = np.moveaxis(np.asarray(x, np.float32).astype(ml_dtypes.bfloat16).astype(np.float64), axis, -1)
    blocks = v.reshape(v.shape[:-1] + (-1, 32))
    amax = np.abs(blocks).max(-1, keepdims=True)
    byte = np.maximum(np.where(amax > 0, np.frexp(amax)[1] - 1 + 127, 0) - down, 1)
    scale = np.exp2(byte - 127.0)
    codes = (blocks / scale).astype(np.float32).astype(dtype).astype(np.float64)
    return np.moveaxis((codes * scale).reshape(v.shape), -1, axis)


WIDE = False


def mx_kscale(k):
    if not WIDE:
        return np.ones(k)
    levels = np.array([10, -10, 5, -5, 0])
    a = np.random.permutation(np.resize(levels, k // 512 * 4)).reshape(k // 512, 4)
    idx = np.arange(k)
    return np.exp2(a[idx // 512, idx % 128 // 32])


BF16 = ml_dtypes.bfloat16


def bf(x):
    return np.asarray(x, np.float32).astype(BF16)


def f64(x):
    return np.asarray(x).astype(np.float64)


E2M1 = np.array([0.0, 0.5, 1.0, 1.5, 2.0, 3.0, 4.0, 6.0, -0.0, -0.5, -1.0, -1.5, -2.0, -3.0, -4.0, -6.0])


def pack_weight(w, fmt):
    k, n = w.shape
    w = f64(bf(w)).reshape(k // 32, 32, n)
    amax = np.abs(w).max(1)
    if fmt == "e4m3":
        byte = np.frexp(amax)[1] - 1 + 127 - 7
    else:
        mant, ex = np.frexp(amax / 6.0)
        byte = np.where(mant > 0.5, ex, ex - 1) + 127
    byte = np.clip(np.where(amax > 0, byte, 1), 1, 254)
    scaled = (w * np.exp2(127.0 - byte)[:, None, :]).reshape(k, n).astype(np.float32)
    by_word = np.ascontiguousarray(scaled.reshape(k // 512, 128, 4, n).transpose(0, 1, 3, 2))
    if fmt == "e4m3":
        words = by_word.astype(ml_dtypes.float8_e4m3fn).view(np.uint8)
    else:
        c = by_word.astype(ml_dtypes.float4_e2m1fn).view(np.uint8) & 0xF
        words = c[..., 0::2] | (c[..., 1::2] << 4)
    return np.ascontiguousarray(words), np.ascontiguousarray(byte.astype(np.uint8).reshape(k // 512, 16, n))


def unpack_weight(words, scales, fmt):
    g, p, n, _ = words.shape
    if fmt == "e4m3":
        vals = np.ascontiguousarray(words).view(ml_dtypes.float8_e4m3fn).astype(np.float64)
    else:
        nib = np.empty((g, p, n, 4), np.uint8)
        nib[..., 0::2] = words & 0xF
        nib[..., 1::2] = words >> 4
        vals = E2M1[nib]
    vals = vals * np.repeat(np.exp2(scales.astype(np.float64) - 127.0), 8, axis=1)[..., None]
    return vals.transpose(0, 1, 3, 2).reshape(g * 512, n)


B, HQ, HK, S, D, HID, BS = 1, 8, 2, 4096, 256, 512, 8
NB = S // BS
G = HQ // HK


def rotate_half(x):
    h = x.shape[-1] // 2
    return np.concatenate([-x[..., h:], x[..., :h]], axis=-1)


def pool_cat(x):
    b, h, s, d = x.shape
    xb = x.reshape(b, h, s // BS, BS, d)
    return np.concatenate([xb.mean(axis=3), xb.max(axis=3)], axis=-1)


def setup_inputs():
    s = mx_kscale(2 * D)[:D]
    s2 = np.concatenate([s, s])
    t = mx_kscale(HID)[:HID // 2]
    t2 = np.concatenate([t, t])
    q = bf(np.random.standard_normal((B, HQ, S, D)) * s)
    k = bf(np.random.standard_normal((B, HK, S, D)) * s)
    wq = np.random.standard_normal((HQ, 2 * D, HID)) * 1.25 / np.sqrt(2 * D) / s2[:, None] * t2
    wk = np.random.standard_normal((HK, 2 * D, HID)) * 1.25 / np.sqrt(2 * D) / s2[:, None] / t2
    wq_words, wq_scales = pack_weight(wq.reshape(-1, HID), "e4m3")
    wk_words, wk_scales = pack_weight(wk.reshape(-1, HID), "e4m3")
    keep = np.random.random((B, 1, NB, NB)) < 0.9
    mask = np.tril(np.ones((NB, NB), bool), 1) & (keep | np.eye(NB, dtype=bool) | np.eye(NB, k=1, dtype=bool))
    pos = np.arange(NB, dtype=np.float64)
    inv_freq = 1.0 / (10000.0 ** (np.arange(0, HID, 2, dtype=np.float64) / HID))
    freqs = pos[:, None] * inv_freq[None, :]
    emb = np.concatenate([freqs, freqs], axis=-1)
    cos = bf(np.broadcast_to(np.cos(emb)[None], (B, NB, HID)))
    sin = bf(np.broadcast_to(np.sin(emb)[None], (B, NB, HID)))
    return {"q": q, "k": k, "attention_mask": mask, "cos": cos, "sin": sin, "wq_words": wq_words, "wq_scales": wq_scales, "wk_words": wk_words, "wk_scales": wk_scales}


def reference(q, k, attention_mask, cos, sin, wq_words, wq_scales, wk_words, wk_scales):
    qh = mxq(pool_cat(f64(q)), 3, "e4m3") @ unpack_weight(wq_words, wq_scales, "e4m3").reshape(HQ, 2 * D, HID)
    kh = mxq(pool_cat(f64(k)), 3, "e4m3") @ unpack_weight(wk_words, wk_scales, "e4m3").reshape(HK, 2 * D, HID)
    c, s = f64(cos)[:, None], f64(sin)[:, None]
    qh = qh * c + rotate_half(qh) * s
    kh = kh * c + rotate_half(kh) * s
    qg = qh.reshape(B, HK, G * NB, HID)
    attn = (mxq(qg, 3, "e4m3") @ mxq(kh.transpose(0, 1, 3, 2), 2, "e4m3")).reshape(B, HQ, NB, NB) / np.sqrt(HID)
    attn = np.where(attention_mask, attn, -1e9)
    e = np.exp(attn - attn.max(axis=-1, keepdims=True))
    return e / e.sum(axis=-1, keepdims=True)

@@ -1,0 +1,211 @@
+import math
+from contextlib import ExitStack
+
+import concourse.mybir as mybir
+from concourse.masks import make_identity
+
+FP8X4 = mybir.dt.float8_e4m3fn_x4
+BF16 = mybir.dt.bfloat16
+F32 = mybir.dt.float32
+I32 = mybir.dt.int32
+U32 = mybir.dt.uint32
+U8 = mybir.dt.uint8
+ALU = mybir.AluOpType
+ACT = mybir.ActivationFunctionType
+AXIS = mybir.AxisListType
+
+P = 128
+PACK = 4
+HQ, HK = 8, 2
+S, D = 4096, 256
+BS = 8
+NB = S // BS
+K = 2 * D
+HID = 512
+HALF = HID // 2
+TILES = NB // P
+MASKED = 1.0e9
+
+FLOPS = 2 * (HQ + HK) * NB * K * HID + 2 * HQ * NB * NB * HID
+
+
+def tile_attngate_e_kernel(
+    tc, q, k, attention_mask, cos, sin, wq_words, wq_scales, wk_words, wk_scales, out
+):
+    nc = tc.nc
+    with ExitStack() as ctx:
+        consts = ctx.enter_context(tc.tile_pool(name="consts", bufs=1))
+        loads = ctx.enter_context(tc.tile_pool(name="loads", bufs=4))
+        trees = ctx.enter_context(tc.tile_pool(name="trees", bufs=2))
+        rows_pool = ctx.enter_context(tc.tile_pool(name="rows", bufs=2))
+        grouped_pool = ctx.enter_context(tc.tile_pool(name="grouped", bufs=3))
+        codes_pool = ctx.enter_context(tc.tile_pool(name="codes", bufs=2))
+        rope_pool = ctx.enter_context(tc.tile_pool(name="rope", bufs=3))
+        soft_pool = ctx.enter_context(tc.tile_pool(name="soft", bufs=3))
+        stats_pool = ctx.enter_context(tc.tile_pool(name="stats", bufs=4))
+        flip_psum = ctx.enter_context(tc.psum_pool(name="flip", bufs=2))
+        proj_psum = ctx.enter_context(tc.psum_pool(name="proj", bufs=3))
+        score_psum = ctx.enter_context(tc.psum_pool(name="score", bufs=3))
+
+        ident = consts.tile([P, P], F32)
+        make_identity(nc, ident[:])
+
+        w_words = consts.tile([P, HK + HQ, HID], I32, align_bytes=64)
+        nc.sync.dma_start(
+            out=w_words[:, 0:HK, :],
+            in_=wk_words.rearrange("g p n t -> p g (n t)").bitcast(I32),
+        )
+        nc.sync.dma_start(
+            out=w_words[:, HK:, :],
+            in_=wq_words.rearrange("g p n t -> p g (n t)").bitcast(I32),
+        )
+        w_scales = consts.tile([P, HK + HQ, HID], U8, align_bytes=64)
+        nc.vector.memset(w_scales[:].bitcast(I32), 0)
+        for quad in range(4):
+            nc.sync.dma_start(
+                out=w_scales[32 * quad : 32 * quad + 4, 0:HK, :].bitcast(I32),
+                in_=wk_scales[:, 4 * quad : 4 * quad + 4, :].rearrange("g r n -> r g n").bitcast(I32),
+            )
+            nc.sync.dma_start(
+                out=w_scales[32 * quad : 32 * quad + 4, HK:, :].bitcast(I32),
+                in_=wq_scales[:, 4 * quad : 4 * quad + 4, :].rearrange("g r n -> r g n").bitcast(I32),
+            )
+
+        cos_sb = consts.tile([P, TILES, HID], BF16)
+        nc.sync.dma_start(out=cos_sb[:], in_=cos[0].rearrange("(c p) h -> p c h", p=P))
+        sin_sb = consts.tile([P, TILES, HID], BF16)
+        nc.sync.dma_start(out=sin_sb[:], in_=sin[0].rearrange("(c p) h -> p c h", p=P))
+        nc.vector.tensor_scalar_mul(sin_sb[:, :, 0:HALF], sin_sb[:, :, 0:HALF], -1.0)
+
+        mask_words = consts.tile([P, TILES, 2 * NB], I32)
+        nc.sync.dma_start(
+            out=mask_words[:],
+            in_=attention_mask.bitcast(I32)[0, 0].rearrange("(c p) w -> p c w", p=P),
+        )
+        mask_bias = consts.tile([P, TILES, NB], F32)
+        nc.vector.tensor_scalar(
+            out=mask_bias[:],
+            in0=mask_words[:].rearrange("p c (j w) -> p c j w", w=2)[:, :, :, 0],
+            scalar1=1.0,
+            scalar2=MASKED,
+            op0=ALU.subtract,
+            op1=ALU.mult,
+        )
+
+        k_codes = consts.tile([P, HK, NB], U32, align_bytes=64)
+        k_scales = consts.tile([P, HK, NB], U8, align_bytes=64)
+
+        def pool_head(x_dram):
+            pooled = rows_pool.tile([P, TILES, K], BF16)
+            for half in range(2):
+                two = slice(2 * half, 2 * half + 2)
+                x = loads.tile([P, 2, BS * D], BF16)
+                nc.sync.dma_start(
+                    out=x[:],
+                    in_=x_dram[S // 2 * half : S // 2 * (half + 1), :].rearrange(
+                        "(c p j) d -> p c (j d)", c=2, p=P
+                    ),
+                )
+                max4 = trees.tile([P, 2, 4 * D], BF16)
+                nc.vector.tensor_tensor(out=max4[:], in0=x[:, :, 0 : 4 * D], in1=x[:, :, 4 * D :], op=ALU.max)
+                max2 = trees.tile([P, 2, 2 * D], BF16)
+                nc.vector.tensor_tensor(out=max2[:], in0=max4[:, :, 0 : 2 * D], in1=max4[:, :, 2 * D :], op=ALU.max)
+                nc.vector.tensor_tensor(out=pooled[:, two, D:], in0=max2[:, :, 0:D], in1=max2[:, :, D:], op=ALU.max)
+                sum4 = trees.tile([P, 2, 4 * D], F32)
+                nc.vector.tensor_tensor(out=sum4[:], in0=x[:, :, 0 : 4 * D], in1=x[:, :, 4 * D :], op=ALU.add)
+                sum2 = trees.tile([P, 2, 2 * D], F32)
+                nc.vector.tensor_tensor(out=sum2[:], in0=sum4[:, :, 0 : 2 * D], in1=sum4[:, :, 2 * D :], op=ALU.add)
+                sum1 = trees.tile([P, 2, D], F32)
+                nc.vector.tensor_tensor(out=sum1[:], in0=sum2[:, :, 0:D], in1=sum2[:, :, D:], op=ALU.add)
+                nc.scalar.activation(out=pooled[:, two, 0:D], in_=sum1[:], func=ACT.Copy, scale=1.0 / BS)
+            return pooled
+
+        def quantise_rows(rows, codes, scales):
+            grouped = grouped_pool.tile([P, NB, PACK], BF16, align_bytes=64)
+            grouped_flat = grouped[:].rearrange("p b t -> p (b t)")
+            pairs = grouped_flat.bitcast(F32).rearrange("p (c b u) -> p c b u", c=TILES, u=2)
+            for half in range(2):
+                flipped = flip_psum.tile([P, 2, 2, P], F32)
+                for c in range(2):
+                    words = rows[:, 2 * half + c, :].bitcast(F32)
+                    for u in range(2):
+                        nc.tensor.transpose(flipped[:, c, u, :], words[:, u : K // 2 : 2], ident[:])
+                nc.scalar.copy(
+                    out=pairs[:, 2 * half : 2 * half + 2, :, :],
+                    in_=flipped[:].rearrange("p c u b -> p c b u"),
+                )
+            nc.vector.quantize_mx(out=codes.bitcast(FP8X4), scales=scales, in_=grouped_flat)
+
+        def project_and_rotate(pooled, head):
+            p_codes = codes_pool.tile([P, NB], U32, align_bytes=64)
+            p_scales = codes_pool.tile([P, NB], U8, align_bytes=64)
+            quantise_rows(pooled[:], p_codes[:], p_scales[:])
+            rotated = rows_pool.tile([P, TILES, HID], BF16)
+            for c in range(TILES):
+                blocks = slice(P * c, P * (c + 1))
+                proj = proj_psum.tile([P, HID], F32)
+                nc.tensor.matmul_mx(
+                    out=proj[:],
+                    lhsT=p_codes[:, blocks].bitcast(FP8X4),
+                    lhsT_scale=p_scales[:, blocks],
+                    rhs=w_words[:, head, :].bitcast(FP8X4),
+                    rhs_scale=w_scales[:, head, :],
+                    start=True,
+                    stop=True,
+                )
+                straight = rope_pool.tile([P, HID], F32)
+                nc.vector.tensor_tensor(out=straight[:], in0=proj[:], in1=cos_sb[:, c, :], op=ALU.mult)
+                crossed = rope_pool.tile([P, HID], F32)
+                nc.vector.tensor_tensor(
+                    out=crossed[:, 0:HALF], in0=proj[:, HALF:], in1=sin_sb[:, c, 0:HALF], op=ALU.mult
+                )
+                nc.vector.tensor_tensor(
+                    out=crossed[:, HALF:], in0=proj[:, 0:HALF], in1=sin_sb[:, c, HALF:], op=ALU.mult
+                )
+                nc.vector.tensor_tensor(out=rotated[:, c, :], in0=straight[:], in1=crossed[:], op=ALU.add)
+            return rotated
+
+        def attend(q_codes, q_scales, kv, out_head):
+            for c in range(TILES):
+                blocks = slice(P * c, P * (c + 1))
+                score = score_psum.tile([P, NB], F32)
+                nc.tensor.matmul_mx(
+                    out=score[:],
+                    lhsT=q_codes[:, blocks].bitcast(FP8X4),
+                    lhsT_scale=q_scales[:, blocks],
+                    rhs=k_codes[:, kv, :].bitcast(FP8X4),
+                    rhs_scale=k_scales[:, kv, :],
+                    start=True,
+                    stop=True,
+                )
+                masked = soft_pool.tile([P, NB], F32)
+                nc.vector.scalar_tensor_tensor(
+                    out=masked[:],
+                    in0=score[:],
+                    scalar=1.0 / math.sqrt(HID),
+                    in1=mask_bias[:, c, :],
+                    op0=ALU.mult,
+                    op1=ALU.add,
+                )
+                neg_max = stats_pool.tile([P, 1], F32)
+                nc.vector.tensor_reduce(out=neg_max[:], in_=masked[:], axis=AXIS.X, op=ALU.max, negate=True)
+                expd = soft_pool.tile([P, NB], F32)
+                total = stats_pool.tile([P, 1], F32)
+                nc.scalar.activation(
+                    out=expd[:], in_=masked[:], func=ACT.Exp, bias=neg_max[:], scale=1.0, accum_out=total[:]
+                )
+                inverse = stats_pool.tile([P, 1], F32)
+                nc.vector.reciprocal(inverse[:], total[:])
+                probs = soft_pool.tile([P, NB], F32)
+                nc.scalar.activation(out=probs[:], in_=expd[:], func=ACT.Copy, scale=inverse[:])
+                nc.scalar.dma_start(out=out_head[blocks, :], in_=probs[:])
+
+        for kv in range(HK):
+            rotated = project_and_rotate(pool_head(k[0, kv]), kv)
+            quantise_rows(rotated[:], k_codes[:, kv, :], k_scales[:, kv, :])
+        for h in range(HQ):
+            rotated = project_and_rotate(pool_head(q[0, h]), HK + h)
+            q_codes = codes_pool.tile([P, NB], U32, align_bytes=64)
+            q_scales = codes_pool.tile([P, NB], U8, align_bytes=64)
+            quantise_rows(rotated[:], q_codes[:], q_scales[:])
+            attend(q_codes, q_scales, h // (HQ // HK), out[0, h])

@@ -24,6 +24,7 @@ K = 2 * D
 HID = 512
 HALF = HID // 2
 TILES = NB // P
+P_BLOCKS = P // BS
 MASKED = 1.0e9
 
 FLOPS = 2 * (HQ + HK) * NB * K * HID + 2 * HQ * NB * NB * HID
@@ -43,81 +44,106 @@ def tile_attngate_e_kernel(
         rope_pool = ctx.enter_context(tc.tile_pool(name="rope", bufs=3))
         soft_pool = ctx.enter_context(tc.tile_pool(name="soft", bufs=3))
         stats_pool = ctx.enter_context(tc.tile_pool(name="stats", bufs=4))
+        mean_psum = ctx.enter_context(tc.psum_pool(name="mean", bufs=2))
         flip_psum = ctx.enter_context(tc.psum_pool(name="flip", bufs=2))
-        proj_psum = ctx.enter_context(tc.psum_pool(name="proj", bufs=3))
-        score_psum = ctx.enter_context(tc.psum_pool(name="score", bufs=3))
+        proj_psum = ctx.enter_context(tc.psum_pool(name="proj", bufs=2))
+        score_psum = ctx.enter_context(tc.psum_pool(name="score", bufs=2))
 
         ident = consts.tile([P, P], F32)
-        make_identity(nc, ident[:])
-
+        ident_bf = consts.tile([P, P], BF16)
+        block_sum = consts.tile([P, P_BLOCKS], F32)
+        block_mean = consts.tile([P, P_BLOCKS], BF16)
         w_words = consts.tile([P, HK + HQ, HID], I32, align_bytes=64)
-        nc.sync.dma_start(
-            out=w_words[:, 0:HK, :],
-            in_=wk_words.rearrange("g p n t -> p g (n t)").bitcast(I32),
-        )
-        nc.sync.dma_start(
-            out=w_words[:, HK:, :],
-            in_=wq_words.rearrange("g p n t -> p g (n t)").bitcast(I32),
-        )
         w_scales = consts.tile([P, HK + HQ, HID], U8, align_bytes=64)
-        nc.vector.memset(w_scales[:].bitcast(I32), 0)
-        for quad in range(4):
-            nc.sync.dma_start(
-                out=w_scales[32 * quad : 32 * quad + 4, 0:HK, :].bitcast(I32),
-                in_=wk_scales[:, 4 * quad : 4 * quad + 4, :].rearrange("g r n -> r g n").bitcast(I32),
-            )
-            nc.sync.dma_start(
-                out=w_scales[32 * quad : 32 * quad + 4, HK:, :].bitcast(I32),
-                in_=wq_scales[:, 4 * quad : 4 * quad + 4, :].rearrange("g r n -> r g n").bitcast(I32),
-            )
-
         cos_sb = consts.tile([P, TILES, HID], BF16)
-        nc.sync.dma_start(out=cos_sb[:], in_=cos[0].rearrange("(c p) h -> p c h", p=P))
         sin_sb = consts.tile([P, TILES, HID], BF16)
-        nc.sync.dma_start(out=sin_sb[:], in_=sin[0].rearrange("(c p) h -> p c h", p=P))
-        nc.vector.tensor_scalar_mul(sin_sb[:, :, 0:HALF], sin_sb[:, :, 0:HALF], -1.0)
-
         mask_words = consts.tile([P, TILES, 2 * NB], I32)
-        nc.sync.dma_start(
-            out=mask_words[:],
-            in_=attention_mask.bitcast(I32)[0, 0].rearrange("(c p) w -> p c w", p=P),
-        )
         mask_bias = consts.tile([P, TILES, NB], F32)
-        nc.vector.tensor_scalar(
-            out=mask_bias[:],
-            in0=mask_words[:].rearrange("p c (j w) -> p c j w", w=2)[:, :, :, 0],
-            scalar1=1.0,
-            scalar2=MASKED,
-            op0=ALU.subtract,
-            op1=ALU.mult,
-        )
-
         k_codes = consts.tile([P, HK, NB], U32, align_bytes=64)
         k_scales = consts.tile([P, HK, NB], U8, align_bytes=64)
 
-        def pool_head(x_dram):
+        make_identity(nc, ident[:])
+        make_identity(nc, ident_bf[:])
+        nc.vector.tensor_reduce(
+            out=block_sum[:], in_=ident[:].rearrange("p (b j) -> p b j", j=BS), axis=AXIS.X, op=ALU.add
+        )
+        nc.vector.tensor_scalar_mul(block_mean[:], block_sum[:], 1.0 / BS)
+        nc.vector.memset(w_scales[:].bitcast(I32), 0)
+
+        def load_head(x_dram):
+            by_block, by_position = [], []
+            for half in range(2):
+                positions = x_dram[S // 2 * half : S // 2 * (half + 1), :]
+                blocks_sb = loads.tile([P, 2, BS * D], BF16)
+                nc.sync.dma_start(
+                    out=blocks_sb[:], in_=positions.rearrange("(c p j) d -> p c (j d)", c=2, p=P)
+                )
+                by_block.append(blocks_sb)
+                positions_sb = loads.tile([P, S // 2 // P, D], BF16)
+                nc.sync.dma_start(out=positions_sb[:], in_=positions.rearrange("(n p) d -> p n d", p=P))
+                by_position.append(positions_sb)
+            return by_block, by_position
+
+        def load_weights(first, count, words, scales):
+            heads = slice(first, first + count)
+            for quad in range(4):
+                nc.sync.dma_start(
+                    out=w_scales[32 * quad : 32 * quad + 4, heads, :].bitcast(I32),
+                    in_=scales[:, 4 * quad : 4 * quad + 4, :].rearrange("g r n -> r g n").bitcast(I32),
+                )
+            nc.sync.dma_start(
+                out=w_words[:, heads, :], in_=words.rearrange("g p n t -> p g (n t)").bitcast(I32)
+            )
+
+        def load_rope_tables():
+            nc.sync.dma_start(out=cos_sb[:], in_=cos[0].rearrange("(c p) h -> p c h", p=P))
+            nc.sync.dma_start(out=sin_sb[:], in_=sin[0].rearrange("(c p) h -> p c h", p=P))
+            nc.vector.tensor_scalar_mul(sin_sb[:, :, 0:HALF], sin_sb[:, :, 0:HALF], -1.0)
+
+        def load_mask():
+            nc.sync.dma_start(
+                out=mask_words[:],
+                in_=attention_mask.bitcast(I32)[0, 0].rearrange("(c p) w -> p c w", p=P),
+            )
+            nc.vector.tensor_scalar(
+                out=mask_bias[:],
+                in0=mask_words[:].rearrange("p c (j w) -> p c j w", w=2)[:, :, :, 0],
+                scalar1=1.0,
+                scalar2=MASKED,
+                op0=ALU.subtract,
+                op1=ALU.mult,
+            )
+
+        def pool_head(by_block, by_position):
             pooled = rows_pool.tile([P, TILES, K], BF16)
             for half in range(2):
                 two = slice(2 * half, 2 * half + 2)
-                x = loads.tile([P, 2, BS * D], BF16)
-                nc.sync.dma_start(
-                    out=x[:],
-                    in_=x_dram[S // 2 * half : S // 2 * (half + 1), :].rearrange(
-                        "(c p j) d -> p c (j d)", c=2, p=P
-                    ),
-                )
+                x = by_block[half]
                 max4 = trees.tile([P, 2, 4 * D], BF16)
                 nc.vector.tensor_tensor(out=max4[:], in0=x[:, :, 0 : 4 * D], in1=x[:, :, 4 * D :], op=ALU.max)
                 max2 = trees.tile([P, 2, 2 * D], BF16)
                 nc.vector.tensor_tensor(out=max2[:], in0=max4[:, :, 0 : 2 * D], in1=max4[:, :, 2 * D :], op=ALU.max)
                 nc.vector.tensor_tensor(out=pooled[:, two, D:], in0=max2[:, :, 0:D], in1=max2[:, :, D:], op=ALU.max)
-                sum4 = trees.tile([P, 2, 4 * D], F32)
-                nc.vector.tensor_tensor(out=sum4[:], in0=x[:, :, 0 : 4 * D], in1=x[:, :, 4 * D :], op=ALU.add)
-                sum2 = trees.tile([P, 2, 2 * D], F32)
-                nc.vector.tensor_tensor(out=sum2[:], in0=sum4[:, :, 0 : 2 * D], in1=sum4[:, :, 2 * D :], op=ALU.add)
-                sum1 = trees.tile([P, 2, D], F32)
-                nc.vector.tensor_tensor(out=sum1[:], in0=sum2[:, :, 0:D], in1=sum2[:, :, D:], op=ALU.add)
-                nc.scalar.activation(out=pooled[:, two, 0:D], in_=sum1[:], func=ACT.Copy, scale=1.0 / BS)
+                x = by_position[half]
+                mean_t = mean_psum.tile([P, 2, 2 * P], F32)
+                for n in range(S // 2 // P):
+                    for f in range(2):
+                        nc.tensor.matmul(
+                            out=mean_t[:, f, P_BLOCKS * n : P_BLOCKS * (n + 1)],
+                            lhsT=x[:, n, P * f : P * (f + 1)],
+                            rhs=block_mean[:],
+                            start=True,
+                            stop=True,
+                        )
+                mean_bf = trees.tile([P, 2, 2 * P], BF16)
+                nc.scalar.copy(out=mean_bf[:], in_=mean_t[:])
+                mean_rows = flip_psum.tile([P, 2, D], BF16, tag="flip")
+                for c in range(2):
+                    for f in range(2):
+                        nc.tensor.transpose(
+                            mean_rows[:, c, P * f : P * (f + 1)], mean_bf[:, f, P * c : P * (c + 1)], ident_bf[:]
+                        )
+                nc.scalar.copy(out=pooled[:, two, 0:D], in_=mean_rows[:])
             return pooled
 
         def quantise_rows(rows, codes, scales):
@@ -125,7 +151,7 @@ def tile_attngate_e_kernel(
             grouped_flat = grouped[:].rearrange("p b t -> p (b t)")
             pairs = grouped_flat.bitcast(F32).rearrange("p (c b u) -> p c b u", c=TILES, u=2)
             for half in range(2):
-                flipped = flip_psum.tile([P, 2, 2, P], F32)
+                flipped = flip_psum.tile([P, 2, 2, P], F32, tag="flip")
                 for c in range(2):
                     words = rows[:, 2 * half + c, :].bitcast(F32)
                     for u in range(2):
@@ -200,12 +226,22 @@ def tile_attngate_e_kernel(
                 nc.scalar.activation(out=probs[:], in_=expd[:], func=ACT.Copy, scale=inverse[:])
                 nc.scalar.dma_start(out=out_head[blocks, :], in_=probs[:])
 
-        for kv in range(HK):
-            rotated = project_and_rotate(pool_head(k[0, kv]), kv)
-            quantise_rows(rotated[:], k_codes[:, kv, :], k_scales[:, kv, :])
-        for h in range(HQ):
-            rotated = project_and_rotate(pool_head(q[0, h]), HK + h)
-            q_codes = codes_pool.tile([P, NB], U32, align_bytes=64)
-            q_scales = codes_pool.tile([P, NB], U8, align_bytes=64)
-            quantise_rows(rotated[:], q_codes[:], q_scales[:])
-            attend(q_codes, q_scales, h // (HQ // HK), out[0, h])
+        heads = [k[0, kv] for kv in range(HK)] + [q[0, h] for h in range(HQ)]
+        loaded = load_head(heads[0])
+        load_weights(0, HK, wk_words, wk_scales)
+        load_rope_tables()
+        for i in range(HK + HQ):
+            current = loaded
+            if i + 1 < HK + HQ:
+                loaded = load_head(heads[i + 1])
+            if i == 0:
+                load_weights(HK, HQ, wq_words, wq_scales)
+                load_mask()
+            rotated = project_and_rotate(pool_head(current[0], current[1]), i)
+            if i < HK:
+                quantise_rows(rotated[:], k_codes[:, i, :], k_scales[:, i, :])
+            else:
+                q_codes = codes_pool.tile([P, NB], U32, align_bytes=64)
+                q_scales = codes_pool.tile([P, NB], U8, align_bytes=64)
+                quantise_rows(rotated[:], q_codes[:], q_scales[:])
+                attend(q_codes, q_scales, (i - HK) // (HQ // HK), out[0, i - HK])

@@ -162,11 +162,8 @@ def tile_attngate_e_kernel(
                 )
             nc.vector.quantize_mx(out=codes.bitcast(FP8X4), scales=scales, in_=grouped_flat)
 
-        def project_and_rotate(pooled, head):
-            p_codes = codes_pool.tile([P, NB], U32, align_bytes=64)
-            p_scales = codes_pool.tile([P, NB], U8, align_bytes=64)
-            quantise_rows(pooled[:], p_codes[:], p_scales[:])
-            rotated = rows_pool.tile([P, TILES, HID], BF16)
+        def project_rotate_quantise(p_codes, p_scales, head, codes, scales):
+            grouped = grouped_pool.tile([P, NB, PACK], BF16, align_bytes=64)
             for c in range(TILES):
                 blocks = slice(P * c, P * (c + 1))
                 proj = proj_psum.tile([P, HID], F32)
@@ -188,8 +185,21 @@ def tile_attngate_e_kernel(
                 nc.vector.tensor_tensor(
                     out=crossed[:, HALF:], in0=proj[:, 0:HALF], in1=sin_sb[:, c, HALF:], op=ALU.mult
                 )
-                nc.vector.tensor_tensor(out=rotated[:, c, :], in0=straight[:], in1=crossed[:], op=ALU.add)
-            return rotated
+                rotated_t = flip_psum.tile([P, PACK, P], F32, tag="flip")
+                for t in range(PACK):
+                    cols = slice(P * t, P * (t + 1))
+                    nc.tensor.matmul(
+                        out=rotated_t[:, t, :], lhsT=straight[:, cols], rhs=ident[:],
+                        is_transpose=True, start=True, stop=False,
+                    )
+                    nc.tensor.matmul(
+                        out=rotated_t[:, t, :], lhsT=crossed[:, cols], rhs=ident[:],
+                        is_transpose=True, start=False, stop=True,
+                    )
+                nc.scalar.copy(out=grouped[:, blocks, :], in_=rotated_t[:].rearrange("p t b -> p b t"))
+            nc.vector.quantize_mx(
+                out=codes.bitcast(FP8X4), scales=scales, in_=grouped[:].rearrange("p b t -> p (b t)")
+            )
 
         def attend(q_codes, q_scales, kv, out_head):
             for c in range(TILES):
@@ -227,21 +237,31 @@ def tile_attngate_e_kernel(
                 nc.scalar.dma_start(out=out_head[blocks, :], in_=probs[:])
 
         heads = [k[0, kv] for kv in range(HK)] + [q[0, h] for h in range(HQ)]
-        loaded = load_head(heads[0])
+        n_heads = HK + HQ
+        loaded, pooled_mx, rotated_mx = {}, {}, {}
+        loaded[0] = load_head(heads[0])
         load_weights(0, HK, wk_words, wk_scales)
         load_rope_tables()
-        for i in range(HK + HQ):
-            current = loaded
-            if i + 1 < HK + HQ:
-                loaded = load_head(heads[i + 1])
-            if i == 0:
+        for step in range(n_heads + 2):
+            if step + 1 < n_heads:
+                loaded[step + 1] = load_head(heads[step + 1])
+            if step == 0:
                 load_weights(HK, HQ, wq_words, wq_scales)
                 load_mask()
-            rotated = project_and_rotate(pool_head(current[0], current[1]), i)
-            if i < HK:
-                quantise_rows(rotated[:], k_codes[:, i, :], k_scales[:, i, :])
-            else:
+            if step < n_heads:
+                pooled = pool_head(loaded[step][0], loaded[step][1])
+                p_codes = codes_pool.tile([P, NB], U32, align_bytes=64)
+                p_scales = codes_pool.tile([P, NB], U8, align_bytes=64)
+                quantise_rows(pooled[:], p_codes[:], p_scales[:])
+                pooled_mx[step] = (p_codes, p_scales)
+            i = step - 1
+            if 0 <= i < HK:
+                project_rotate_quantise(pooled_mx[i][0], pooled_mx[i][1], i, k_codes[:, i, :], k_scales[:, i, :])
+            if HK <= i < n_heads:
                 q_codes = codes_pool.tile([P, NB], U32, align_bytes=64)
                 q_scales = codes_pool.tile([P, NB], U8, align_bytes=64)
-                quantise_rows(rotated[:], q_codes[:], q_scales[:])
-                attend(q_codes, q_scales, (i - HK) // (HQ // HK), out[0, i - HK])
+                project_rotate_quantise(pooled_mx[i][0], pooled_mx[i][1], i, q_codes[:], q_scales[:])
+                rotated_mx[i] = (q_codes, q_scales)
+            i = step - 2
+            if HK <= i:
+                attend(rotated_mx[i][0], rotated_mx[i][1], (i - HK) // (HQ // HK), out[0, i - HK])

@@ -27,6 +27,13 @@ TILES = NB // P
 P_BLOCKS = P // BS
 MASKED = 1.0e9
 
+UNIT_TILES = 2
+UNIT_BLOCKS = UNIT_TILES * P
+UNIT_POSITIONS = UNIT_BLOCKS * BS
+UNITS = TILES // UNIT_TILES
+LOADS_AHEAD = 3
+STORE_LAG = 8
+
 FLOPS = 2 * (HQ + HK) * NB * K * HID + 2 * HQ * NB * NB * HID
 
 
@@ -36,13 +43,14 @@ def tile_attngate_e_kernel(
     nc = tc.nc
     with ExitStack() as ctx:
         consts = ctx.enter_context(tc.tile_pool(name="consts", bufs=1))
-        loads = ctx.enter_context(tc.tile_pool(name="loads", bufs=4))
+        loads = ctx.enter_context(tc.tile_pool(name="loads", bufs=LOADS_AHEAD + 1))
         trees = ctx.enter_context(tc.tile_pool(name="trees", bufs=2))
         rows_pool = ctx.enter_context(tc.tile_pool(name="rows", bufs=2))
         grouped_pool = ctx.enter_context(tc.tile_pool(name="grouped", bufs=3))
         codes_pool = ctx.enter_context(tc.tile_pool(name="codes", bufs=2))
         rope_pool = ctx.enter_context(tc.tile_pool(name="rope", bufs=3))
         soft_pool = ctx.enter_context(tc.tile_pool(name="soft", bufs=3))
+        probs_pool = ctx.enter_context(tc.tile_pool(name="probs", bufs=STORE_LAG + 2))
         stats_pool = ctx.enter_context(tc.tile_pool(name="stats", bufs=4))
         mean_psum = ctx.enter_context(tc.psum_pool(name="mean", bufs=2))
         flip_psum = ctx.enter_context(tc.psum_pool(name="flip", bufs=2))
@@ -70,29 +78,28 @@ def tile_attngate_e_kernel(
         nc.vector.tensor_scalar_mul(block_mean[:], block_sum[:], 1.0 / BS)
         nc.vector.memset(w_scales[:].bitcast(I32), 0)
 
-        def load_head(x_dram):
-            by_block, by_position = [], []
-            for half in range(2):
-                positions = x_dram[S // 2 * half : S // 2 * (half + 1), :]
-                blocks_sb = loads.tile([P, 2, BS * D], BF16)
-                nc.sync.dma_start(
-                    out=blocks_sb[:], in_=positions.rearrange("(c p j) d -> p c (j d)", c=2, p=P)
-                )
-                by_block.append(blocks_sb)
-                positions_sb = loads.tile([P, S // 2 // P, D], BF16)
-                nc.sync.dma_start(out=positions_sb[:], in_=positions.rearrange("(n p) d -> p n d", p=P))
-                by_position.append(positions_sb)
-            return by_block, by_position
+        heads = [k[0, kv] for kv in range(HK)] + [q[0, h] for h in range(HQ)]
+
+        def load_unit(unit):
+            head, part = divmod(unit, UNITS)
+            positions = heads[head][UNIT_POSITIONS * part : UNIT_POSITIONS * (part + 1), :]
+            by_position = loads.tile([P, UNIT_POSITIONS // P, D], BF16)
+            nc.sync.dma_start(out=by_position[:], in_=positions.rearrange("(n p) d -> p n d", p=P))
+            by_block = loads.tile([P, UNIT_TILES, BS * D], BF16)
+            nc.sync.dma_start(
+                out=by_block[:], in_=positions.rearrange("(c p j) d -> p c (j d)", c=UNIT_TILES, p=P)
+            )
+            return by_position, by_block
 
         def load_weights(first, count, words, scales):
-            heads = slice(first, first + count)
+            some = slice(first, first + count)
             for quad in range(4):
                 nc.sync.dma_start(
-                    out=w_scales[32 * quad : 32 * quad + 4, heads, :].bitcast(I32),
+                    out=w_scales[32 * quad : 32 * quad + 4, some, :].bitcast(I32),
                     in_=scales[:, 4 * quad : 4 * quad + 4, :].rearrange("g r n -> r g n").bitcast(I32),
                 )
             nc.sync.dma_start(
-                out=w_words[:, heads, :], in_=words.rearrange("g p n t -> p g (n t)").bitcast(I32)
+                out=w_words[:, some, :], in_=words.rearrange("g p n t -> p g (n t)").bitcast(I32)
             )
 
         def load_rope_tables():
@@ -114,58 +121,59 @@ def tile_attngate_e_kernel(
                 op1=ALU.mult,
             )
 
-        def pool_head(by_block, by_position):
-            pooled = rows_pool.tile([P, TILES, K], BF16)
-            for half in range(2):
-                two = slice(2 * half, 2 * half + 2)
-                x = by_block[half]
-                max4 = trees.tile([P, 2, 4 * D], BF16)
-                nc.vector.tensor_tensor(out=max4[:], in0=x[:, :, 0 : 4 * D], in1=x[:, :, 4 * D :], op=ALU.max)
-                max2 = trees.tile([P, 2, 2 * D], BF16)
-                nc.vector.tensor_tensor(out=max2[:], in0=max4[:, :, 0 : 2 * D], in1=max4[:, :, 2 * D :], op=ALU.max)
-                nc.vector.tensor_tensor(out=pooled[:, two, D:], in0=max2[:, :, 0:D], in1=max2[:, :, D:], op=ALU.max)
-                x = by_position[half]
-                mean_t = mean_psum.tile([P, 2, 2 * P], F32)
-                for n in range(S // 2 // P):
-                    for f in range(2):
-                        nc.tensor.matmul(
-                            out=mean_t[:, f, P_BLOCKS * n : P_BLOCKS * (n + 1)],
-                            lhsT=x[:, n, P * f : P * (f + 1)],
-                            rhs=block_mean[:],
-                            start=True,
-                            stop=True,
-                        )
-                mean_bf = trees.tile([P, 2, 2 * P], BF16)
-                nc.scalar.copy(out=mean_bf[:], in_=mean_t[:])
-                mean_rows = flip_psum.tile([P, 2, D], BF16, tag="flip")
-                for c in range(2):
-                    for f in range(2):
-                        nc.tensor.transpose(
-                            mean_rows[:, c, P * f : P * (f + 1)], mean_bf[:, f, P * c : P * (c + 1)], ident_bf[:]
-                        )
-                nc.scalar.copy(out=pooled[:, two, 0:D], in_=mean_rows[:])
+        def pool_unit(by_position, by_block):
+            pooled = rows_pool.tile([P, UNIT_TILES, K], BF16)
+            mean_t = mean_psum.tile([P, 2, UNIT_BLOCKS], F32)
+            for n in range(UNIT_POSITIONS // P):
+                for f in range(2):
+                    nc.tensor.matmul(
+                        out=mean_t[:, f, P_BLOCKS * n : P_BLOCKS * (n + 1)],
+                        lhsT=by_position[:, n, P * f : P * (f + 1)],
+                        rhs=block_mean[:],
+                        start=True,
+                        stop=True,
+                    )
+            mean_bf = trees.tile([P, 2, UNIT_BLOCKS], BF16)
+            nc.scalar.copy(out=mean_bf[:], in_=mean_t[:])
+            mean_rows = flip_psum.tile([P, UNIT_TILES, D], BF16, tag="flip")
+            for c in range(UNIT_TILES):
+                for f in range(2):
+                    nc.tensor.transpose(
+                        mean_rows[:, c, P * f : P * (f + 1)], mean_bf[:, f, P * c : P * (c + 1)], ident_bf[:]
+                    )
+            nc.scalar.copy(out=pooled[:, :, 0:D], in_=mean_rows[:])
+            max4 = trees.tile([P, UNIT_TILES, 4 * D], BF16)
+            nc.vector.tensor_tensor(
+                out=max4[:], in0=by_block[:, :, 0 : 4 * D], in1=by_block[:, :, 4 * D :], op=ALU.max
+            )
+            max2 = trees.tile([P, UNIT_TILES, 2 * D], BF16)
+            nc.vector.tensor_tensor(out=max2[:], in0=max4[:, :, 0 : 2 * D], in1=max4[:, :, 2 * D :], op=ALU.max)
+            nc.vector.tensor_tensor(out=pooled[:, :, D:], in0=max2[:, :, 0:D], in1=max2[:, :, D:], op=ALU.max)
             return pooled
 
-        def quantise_rows(rows, codes, scales):
-            grouped = grouped_pool.tile([P, NB, PACK], BF16, align_bytes=64)
+        def quantise_pooled(pooled):
+            grouped = grouped_pool.tile([P, UNIT_BLOCKS, PACK], BF16, align_bytes=64)
             grouped_flat = grouped[:].rearrange("p b t -> p (b t)")
-            pairs = grouped_flat.bitcast(F32).rearrange("p (c b u) -> p c b u", c=TILES, u=2)
-            for half in range(2):
-                flipped = flip_psum.tile([P, 2, 2, P], F32, tag="flip")
-                for c in range(2):
-                    words = rows[:, 2 * half + c, :].bitcast(F32)
-                    for u in range(2):
-                        nc.tensor.transpose(flipped[:, c, u, :], words[:, u : K // 2 : 2], ident[:])
-                nc.scalar.copy(
-                    out=pairs[:, 2 * half : 2 * half + 2, :, :],
-                    in_=flipped[:].rearrange("p c u b -> p c b u"),
-                )
-            nc.vector.quantize_mx(out=codes.bitcast(FP8X4), scales=scales, in_=grouped_flat)
+            flipped = flip_psum.tile([P, UNIT_TILES, 2, P], F32, tag="flip")
+            for c in range(UNIT_TILES):
+                words = pooled[:, c, :].bitcast(F32)
+                for u in range(2):
+                    nc.tensor.transpose(flipped[:, c, u, :], words[:, u : K // 2 : 2], ident[:])
+            nc.scalar.copy(
+                out=grouped_flat.bitcast(F32).rearrange("p (c b u) -> p c b u", c=UNIT_TILES, u=2),
+                in_=flipped[:].rearrange("p c u b -> p c b u"),
+            )
+            p_codes = codes_pool.tile([P, UNIT_BLOCKS], U32, align_bytes=64)
+            p_scales = codes_pool.tile([P, UNIT_BLOCKS], U8, align_bytes=64)
+            nc.vector.quantize_mx(out=p_codes[:].bitcast(FP8X4), scales=p_scales[:], in_=grouped_flat)
+            return p_codes, p_scales
 
-        def project_rotate_quantise(p_codes, p_scales, head, codes, scales):
-            grouped = grouped_pool.tile([P, NB, PACK], BF16, align_bytes=64)
-            for c in range(TILES):
+        def project_rotate_quantise(p_codes, p_scales, unit, codes, scales):
+            head, part = divmod(unit, UNITS)
+            grouped = grouped_pool.tile([P, UNIT_BLOCKS, PACK], BF16, align_bytes=64)
+            for c in range(UNIT_TILES):
                 blocks = slice(P * c, P * (c + 1))
+                tile_in_head = UNIT_TILES * part + c
                 proj = proj_psum.tile([P, HID], F32)
                 nc.tensor.matmul_mx(
                     out=proj[:],
@@ -177,13 +185,13 @@ def tile_attngate_e_kernel(
                     stop=True,
                 )
                 straight = rope_pool.tile([P, HID], F32)
-                nc.vector.tensor_tensor(out=straight[:], in0=proj[:], in1=cos_sb[:, c, :], op=ALU.mult)
+                nc.vector.tensor_tensor(out=straight[:], in0=proj[:], in1=cos_sb[:, tile_in_head, :], op=ALU.mult)
                 crossed = rope_pool.tile([P, HID], F32)
                 nc.vector.tensor_tensor(
-                    out=crossed[:, 0:HALF], in0=proj[:, HALF:], in1=sin_sb[:, c, 0:HALF], op=ALU.mult
+                    out=crossed[:, 0:HALF], in0=proj[:, HALF:], in1=sin_sb[:, tile_in_head, 0:HALF], op=ALU.mult
                 )
                 nc.vector.tensor_tensor(
-                    out=crossed[:, HALF:], in0=proj[:, 0:HALF], in1=sin_sb[:, c, HALF:], op=ALU.mult
+                    out=crossed[:, HALF:], in0=proj[:, 0:HALF], in1=sin_sb[:, tile_in_head, HALF:], op=ALU.mult
                 )
                 rotated_t = flip_psum.tile([P, PACK, P], F32, tag="flip")
                 for t in range(PACK):
@@ -201,8 +209,11 @@ def tile_attngate_e_kernel(
                 out=codes.bitcast(FP8X4), scales=scales, in_=grouped[:].rearrange("p b t -> p (b t)")
             )
 
-        def attend(q_codes, q_scales, kv, out_head):
-            for c in range(TILES):
+        def attend(q_codes, q_scales, unit):
+            head, part = divmod(unit, UNITS)
+            kv = (head - HK) // (HQ // HK)
+            probs = probs_pool.tile([P, UNIT_TILES, NB], F32)
+            for c in range(UNIT_TILES):
                 blocks = slice(P * c, P * (c + 1))
                 score = score_psum.tile([P, NB], F32)
                 nc.tensor.matmul_mx(
@@ -219,49 +230,57 @@ def tile_attngate_e_kernel(
                     out=masked[:],
                     in0=score[:],
                     scalar=1.0 / math.sqrt(HID),
-                    in1=mask_bias[:, c, :],
+                    in1=mask_bias[:, UNIT_TILES * part + c, :],
                     op0=ALU.mult,
                     op1=ALU.add,
                 )
                 neg_max = stats_pool.tile([P, 1], F32)
                 nc.vector.tensor_reduce(out=neg_max[:], in_=masked[:], axis=AXIS.X, op=ALU.max, negate=True)
-                expd = soft_pool.tile([P, NB], F32)
                 total = stats_pool.tile([P, 1], F32)
                 nc.scalar.activation(
-                    out=expd[:], in_=masked[:], func=ACT.Exp, bias=neg_max[:], scale=1.0, accum_out=total[:]
+                    out=probs[:, c, :], in_=masked[:], func=ACT.Exp, bias=neg_max[:], scale=1.0, accum_out=total[:]
                 )
                 inverse = stats_pool.tile([P, 1], F32)
                 nc.vector.reciprocal(inverse[:], total[:])
-                probs = soft_pool.tile([P, NB], F32)
-                nc.scalar.activation(out=probs[:], in_=expd[:], func=ACT.Copy, scale=inverse[:])
-                nc.scalar.dma_start(out=out_head[blocks, :], in_=probs[:])
+                nc.scalar.activation(out=probs[:, c, :], in_=probs[:, c, :], func=ACT.Copy, scale=inverse[:])
+            return probs
 
-        heads = [k[0, kv] for kv in range(HK)] + [q[0, h] for h in range(HQ)]
-        n_heads = HK + HQ
-        loaded, pooled_mx, rotated_mx = {}, {}, {}
-        loaded[0] = load_head(heads[0])
+        def store(probs, unit):
+            head, part = divmod(unit, UNITS)
+            rows = out[0, head - HK, UNIT_BLOCKS * part : UNIT_BLOCKS * (part + 1), :]
+            nc.sync.dma_start(out=rows.rearrange("(c p) j -> p c j", p=P), in_=probs[:])
+
+        n_units = (HK + HQ) * UNITS
+        key_units = HK * UNITS
+        loaded, pooled_mx, rotated_mx, finished = {}, {}, {}, {}
+        loaded[0] = load_unit(0)
+        loaded[1] = load_unit(1)
         load_weights(0, HK, wk_words, wk_scales)
         load_rope_tables()
-        for step in range(n_heads + 2):
-            if step + 1 < n_heads:
-                loaded[step + 1] = load_head(heads[step + 1])
+        loaded[2] = load_unit(2)
+        for step in range(n_units + 2 + STORE_LAG):
+            if step + LOADS_AHEAD < n_units:
+                loaded[step + LOADS_AHEAD] = load_unit(step + LOADS_AHEAD)
             if step == 0:
                 load_weights(HK, HQ, wq_words, wq_scales)
                 load_mask()
-            if step < n_heads:
-                pooled = pool_head(loaded[step][0], loaded[step][1])
-                p_codes = codes_pool.tile([P, NB], U32, align_bytes=64)
-                p_scales = codes_pool.tile([P, NB], U8, align_bytes=64)
-                quantise_rows(pooled[:], p_codes[:], p_scales[:])
-                pooled_mx[step] = (p_codes, p_scales)
-            i = step - 1
-            if 0 <= i < HK:
-                project_rotate_quantise(pooled_mx[i][0], pooled_mx[i][1], i, k_codes[:, i, :], k_scales[:, i, :])
-            if HK <= i < n_heads:
-                q_codes = codes_pool.tile([P, NB], U32, align_bytes=64)
-                q_scales = codes_pool.tile([P, NB], U8, align_bytes=64)
-                project_rotate_quantise(pooled_mx[i][0], pooled_mx[i][1], i, q_codes[:], q_scales[:])
-                rotated_mx[i] = (q_codes, q_scales)
-            i = step - 2
-            if HK <= i:
-                attend(rotated_mx[i][0], rotated_mx[i][1], (i - HK) // (HQ // HK), out[0, i - HK])
+            if step < n_units:
+                pooled_mx[step] = quantise_pooled(pool_unit(loaded[step][0], loaded[step][1]))
+            unit = step - 1
+            if 0 <= unit < key_units:
+                head, part = divmod(unit, UNITS)
+                some = slice(UNIT_BLOCKS * part, UNIT_BLOCKS * (part + 1))
+                project_rotate_quantise(
+                    pooled_mx[unit][0], pooled_mx[unit][1], unit, k_codes[:, head, some], k_scales[:, head, some]
+                )
+            if key_units <= unit < n_units:
+                q_codes = codes_pool.tile([P, UNIT_BLOCKS], U32, align_bytes=64)
+                q_scales = codes_pool.tile([P, UNIT_BLOCKS], U8, align_bytes=64)
+                project_rotate_quantise(pooled_mx[unit][0], pooled_mx[unit][1], unit, q_codes[:], q_scales[:])
+                rotated_mx[unit] = (q_codes, q_scales)
+            unit = step - 2
+            if key_units <= unit < n_units:
+                finished[unit] = attend(rotated_mx[unit][0], rotated_mx[unit][1], unit)
+            unit = step - 2 - STORE_LAG
+            if key_units <= unit < n_units:
+                store(finished[unit], unit)

@@ -17,6 +17,7 @@ AXIS = mybir.AxisListType
 P = 128
 PACK = 4
 HQ, HK = 8, 2
+GROUP = HQ // HK
 S, D = 4096, 256
 BS = 8
 NB = S // BS
@@ -80,8 +81,7 @@ def tile_attngate_e_kernel(
 
         heads = [k[0, kv] for kv in range(HK)] + [q[0, h] for h in range(HQ)]
 
-        def load_unit(unit):
-            head, part = divmod(unit, UNITS)
+        def load_unit(head, part):
             positions = heads[head][UNIT_POSITIONS * part : UNIT_POSITIONS * (part + 1), :]
             by_position = loads.tile([P, UNIT_POSITIONS // P, D], BF16)
             nc.sync.dma_start(out=by_position[:], in_=positions.rearrange("(n p) d -> p n d", p=P))
@@ -89,18 +89,18 @@ def tile_attngate_e_kernel(
             nc.sync.dma_start(
                 out=by_block[:], in_=positions.rearrange("(c p j) d -> p c (j d)", c=UNIT_TILES, p=P)
             )
+            if part == 0:
+                words = wk_words[head] if head < HK else wq_words[head - HK]
+                nc.sync.dma_start(out=w_words[:, head, :], in_=words.rearrange("p n t -> p (n t)").bitcast(I32))
             return by_position, by_block
 
-        def load_weights(first, count, words, scales):
+        def load_scales(first, count, scales):
             some = slice(first, first + count)
             for quad in range(4):
                 nc.sync.dma_start(
                     out=w_scales[32 * quad : 32 * quad + 4, some, :].bitcast(I32),
                     in_=scales[:, 4 * quad : 4 * quad + 4, :].rearrange("g r n -> r g n").bitcast(I32),
                 )
-            nc.sync.dma_start(
-                out=w_words[:, some, :], in_=words.rearrange("g p n t -> p g (n t)").bitcast(I32)
-            )
 
         def load_rope_tables():
             nc.sync.dma_start(out=cos_sb[:], in_=cos[0].rearrange("(c p) h -> p c h", p=P))
@@ -168,8 +168,7 @@ def tile_attngate_e_kernel(
             nc.vector.quantize_mx(out=p_codes[:].bitcast(FP8X4), scales=p_scales[:], in_=grouped_flat)
             return p_codes, p_scales
 
-        def project_rotate_quantise(p_codes, p_scales, unit, codes, scales):
-            head, part = divmod(unit, UNITS)
+        def project_rotate_quantise(p_codes, p_scales, head, part, codes, scales):
             grouped = grouped_pool.tile([P, UNIT_BLOCKS, PACK], BF16, align_bytes=64)
             for c in range(UNIT_TILES):
                 blocks = slice(P * c, P * (c + 1))
@@ -209,9 +208,8 @@ def tile_attngate_e_kernel(
                 out=codes.bitcast(FP8X4), scales=scales, in_=grouped[:].rearrange("p b t -> p (b t)")
             )
 
-        def attend(q_codes, q_scales, unit):
-            head, part = divmod(unit, UNITS)
-            kv = (head - HK) // (HQ // HK)
+        def attend(q_codes, q_scales, head, part):
+            kv = (head - HK) // GROUP
             probs = probs_pool.tile([P, UNIT_TILES, NB], F32)
             for c in range(UNIT_TILES):
                 blocks = slice(P * c, P * (c + 1))
@@ -245,42 +243,47 @@ def tile_attngate_e_kernel(
                 nc.scalar.activation(out=probs[:, c, :], in_=probs[:, c, :], func=ACT.Copy, scale=inverse[:])
             return probs
 
-        def store(probs, unit):
-            head, part = divmod(unit, UNITS)
+        def store(probs, head, part):
             rows = out[0, head - HK, UNIT_BLOCKS * part : UNIT_BLOCKS * (part + 1), :]
             nc.sync.dma_start(out=rows.rearrange("(c p) j -> p c j", p=P), in_=probs[:])
 
-        n_units = (HK + HQ) * UNITS
-        key_units = HK * UNITS
+        units = []
+        for kv in range(HK):
+            for head in [kv] + [HK + GROUP * kv + g for g in range(GROUP)]:
+                for part in range(UNITS):
+                    units.append((head, part))
+        n_units = len(units)
         loaded, pooled_mx, rotated_mx, finished = {}, {}, {}, {}
-        loaded[0] = load_unit(0)
-        loaded[1] = load_unit(1)
-        load_weights(0, HK, wk_words, wk_scales)
+        loaded[0] = load_unit(units[0][0], units[0][1])
+        load_scales(0, HK, wk_scales)
+        load_scales(HK, HQ, wq_scales)
         load_rope_tables()
-        loaded[2] = load_unit(2)
+        loaded[1] = load_unit(units[1][0], units[1][1])
+        loaded[2] = load_unit(units[2][0], units[2][1])
+        load_mask()
         for step in range(n_units + 2 + STORE_LAG):
-            if step + LOADS_AHEAD < n_units:
-                loaded[step + LOADS_AHEAD] = load_unit(step + LOADS_AHEAD)
-            if step == 0:
-                load_weights(HK, HQ, wq_words, wq_scales)
-                load_mask()
-            if step < n_units:
-                pooled_mx[step] = quantise_pooled(pool_unit(loaded[step][0], loaded[step][1]))
-            unit = step - 1
-            if 0 <= unit < key_units:
-                head, part = divmod(unit, UNITS)
-                some = slice(UNIT_BLOCKS * part, UNIT_BLOCKS * (part + 1))
-                project_rotate_quantise(
-                    pooled_mx[unit][0], pooled_mx[unit][1], unit, k_codes[:, head, some], k_scales[:, head, some]
-                )
-            if key_units <= unit < n_units:
-                q_codes = codes_pool.tile([P, UNIT_BLOCKS], U32, align_bytes=64)
-                q_scales = codes_pool.tile([P, UNIT_BLOCKS], U8, align_bytes=64)
-                project_rotate_quantise(pooled_mx[unit][0], pooled_mx[unit][1], unit, q_codes[:], q_scales[:])
-                rotated_mx[unit] = (q_codes, q_scales)
-            unit = step - 2
-            if key_units <= unit < n_units:
-                finished[unit] = attend(rotated_mx[unit][0], rotated_mx[unit][1], unit)
-            unit = step - 2 - STORE_LAG
-            if key_units <= unit < n_units:
-                store(finished[unit], unit)
+            i = step + LOADS_AHEAD
+            if i < n_units:
+                loaded[i] = load_unit(units[i][0], units[i][1])
+            i = step
+            if i < n_units:
+                pooled_mx[i] = quantise_pooled(pool_unit(loaded[i][0], loaded[i][1]))
+            i = step - 1
+            if 0 <= i < n_units:
+                head, part = units[i]
+                if head < HK:
+                    some = slice(UNIT_BLOCKS * part, UNIT_BLOCKS * (part + 1))
+                    project_rotate_quantise(
+                        pooled_mx[i][0], pooled_mx[i][1], head, part, k_codes[:, head, some], k_scales[:, head, some]
+                    )
+                else:
+                    q_codes = codes_pool.tile([P, UNIT_BLOCKS], U32, align_bytes=64)
+                    q_scales = codes_pool.tile([P, UNIT_BLOCKS], U8, align_bytes=64)
+                    project_rotate_quantise(pooled_mx[i][0], pooled_mx[i][1], head, part, q_codes[:], q_scales[:])
+                    rotated_mx[i] = (q_codes, q_scales)
+            i = step - 2
+            if 0 <= i < n_units and units[i][0] >= HK:
+                finished[i] = attend(rotated_mx[i][0], rotated_mx[i][1], units[i][0], units[i][1])
+            i = step - 2 - STORE_LAG
+            if 0 <= i < n_units and units[i][0] >= HK:
+                store(finished[i], units[i][0], units[i][1])

@@ -60,12 +60,10 @@ def tile_attngate_e_kernel(
 
         ident = consts.tile([P, P], F32)
         ident_bf = consts.tile([P, P], BF16)
-        block_sum = consts.tile([P, P_BLOCKS], F32)
         block_mean = consts.tile([P, P_BLOCKS], BF16)
         w_words = consts.tile([P, HK + HQ, HID], I32, align_bytes=64)
         w_scales = consts.tile([P, HK + HQ, HID], U8, align_bytes=64)
-        cos_sb = consts.tile([P, TILES, HID], BF16)
-        sin_sb = consts.tile([P, TILES, HID], BF16)
+        rope = consts.tile([P, TILES, 2, HID], BF16)
         mask_words = consts.tile([P, TILES, 2 * NB], I32)
         mask_bias = consts.tile([P, TILES, NB], F32)
         k_codes = consts.tile([P, HK, NB], U32, align_bytes=64)
@@ -73,10 +71,15 @@ def tile_attngate_e_kernel(
 
         make_identity(nc, ident[:])
         make_identity(nc, ident_bf[:])
-        nc.vector.tensor_reduce(
-            out=block_sum[:], in_=ident[:].rearrange("p (b j) -> p b j", j=BS), axis=AXIS.X, op=ALU.add
+        nc.gpsimd.memset(block_mean[:], 1.0 / BS)
+        nc.gpsimd.affine_select(
+            out=block_mean[:], in_=block_mean[:], compare_op=ALU.is_ge, fill=0.0,
+            base=0, pattern=[[-BS, P_BLOCKS]], channel_multiplier=1,
         )
-        nc.vector.tensor_scalar_mul(block_mean[:], block_sum[:], 1.0 / BS)
+        nc.gpsimd.affine_select(
+            out=block_mean[:], in_=block_mean[:], compare_op=ALU.is_ge, fill=0.0,
+            base=BS - 1, pattern=[[BS, P_BLOCKS]], channel_multiplier=-1,
+        )
         nc.vector.memset(w_scales[:].bitcast(I32), 0)
 
         heads = [k[0, kv] for kv in range(HK)] + [q[0, h] for h in range(HQ)]
@@ -103,9 +106,12 @@ def tile_attngate_e_kernel(
                 )
 
         def load_rope_tables():
-            nc.sync.dma_start(out=cos_sb[:], in_=cos[0].rearrange("(c p) h -> p c h", p=P))
-            nc.sync.dma_start(out=sin_sb[:], in_=sin[0].rearrange("(c p) h -> p c h", p=P))
-            nc.vector.tensor_scalar_mul(sin_sb[:, :, 0:HALF], sin_sb[:, :, 0:HALF], -1.0)
+            cos_rows = cos[0].rearrange("(c p) h -> p c h", p=P)
+            sin_rows = sin[0].rearrange("(c p) h -> p c h", p=P)
+            nc.sync.dma_start(out=rope[:, :, 0, :], in_=cos_rows)
+            nc.sync.dma_start(out=rope[:, :, 1, 0:HALF], in_=sin_rows[:, :, HALF:])
+            nc.sync.dma_start(out=rope[:, :, 1, HALF:], in_=sin_rows[:, :, 0:HALF])
+            nc.vector.tensor_scalar_mul(rope[:, :, 1, HALF:], rope[:, :, 1, HALF:], -1.0)
 
         def load_mask():
             nc.sync.dma_start(
@@ -183,24 +189,23 @@ def tile_attngate_e_kernel(
                     start=True,
                     stop=True,
                 )
-                straight = rope_pool.tile([P, HID], F32)
-                nc.vector.tensor_tensor(out=straight[:], in0=proj[:], in1=cos_sb[:, tile_in_head, :], op=ALU.mult)
-                crossed = rope_pool.tile([P, HID], F32)
+                products = rope_pool.tile([P, 2, HID], F32)
                 nc.vector.tensor_tensor(
-                    out=crossed[:, 0:HALF], in0=proj[:, HALF:], in1=sin_sb[:, tile_in_head, 0:HALF], op=ALU.mult
-                )
-                nc.vector.tensor_tensor(
-                    out=crossed[:, HALF:], in0=proj[:, 0:HALF], in1=sin_sb[:, tile_in_head, HALF:], op=ALU.mult
+                    out=products[:],
+                    in0=proj[:].unsqueeze(1).to_broadcast([P, 2, HID]),
+                    in1=rope[:, tile_in_head, :, :],
+                    op=ALU.mult,
                 )
                 rotated_t = flip_psum.tile([P, PACK, P], F32, tag="flip")
                 for t in range(PACK):
                     cols = slice(P * t, P * (t + 1))
+                    swapped = (P * t + HALF) % HID
                     nc.tensor.matmul(
-                        out=rotated_t[:, t, :], lhsT=straight[:, cols], rhs=ident[:],
+                        out=rotated_t[:, t, :], lhsT=products[:, 0, cols], rhs=ident[:],
                         is_transpose=True, start=True, stop=False,
                     )
                     nc.tensor.matmul(
-                        out=rotated_t[:, t, :], lhsT=crossed[:, cols], rhs=ident[:],
+                        out=rotated_t[:, t, :], lhsT=products[:, 1, swapped : swapped + P], rhs=ident[:],
                         is_transpose=True, start=False, stop=True,
                     )
                 nc.scalar.copy(out=grouped[:, blocks, :], in_=rotated_t[:].rearrange("p t b -> p b t"))
@@ -211,6 +216,7 @@ def tile_attngate_e_kernel(
         def attend(q_codes, q_scales, head, part):
             kv = (head - HK) // GROUP
             probs = probs_pool.tile([P, UNIT_TILES, NB], F32)
+            masked = soft_pool.tile([P, UNIT_TILES, NB], F32)
             for c in range(UNIT_TILES):
                 blocks = slice(P * c, P * (c + 1))
                 score = score_psum.tile([P, NB], F32)
@@ -223,24 +229,28 @@ def tile_attngate_e_kernel(
                     start=True,
                     stop=True,
                 )
-                masked = soft_pool.tile([P, NB], F32)
                 nc.vector.scalar_tensor_tensor(
-                    out=masked[:],
+                    out=masked[:, c, :],
                     in0=score[:],
                     scalar=1.0 / math.sqrt(HID),
                     in1=mask_bias[:, UNIT_TILES * part + c, :],
                     op0=ALU.mult,
                     op1=ALU.add,
                 )
-                neg_max = stats_pool.tile([P, 1], F32)
-                nc.vector.tensor_reduce(out=neg_max[:], in_=masked[:], axis=AXIS.X, op=ALU.max, negate=True)
-                total = stats_pool.tile([P, 1], F32)
+            neg_max = stats_pool.tile([P, UNIT_TILES], F32)
+            nc.vector.tensor_reduce(out=neg_max[:], in_=masked[:], axis=AXIS.X, op=ALU.max, negate=True)
+            total = stats_pool.tile([P, UNIT_TILES], F32)
+            for c in range(UNIT_TILES):
                 nc.scalar.activation(
-                    out=probs[:, c, :], in_=masked[:], func=ACT.Exp, bias=neg_max[:], scale=1.0, accum_out=total[:]
+                    out=probs[:, c, :], in_=masked[:, c, :], func=ACT.Exp,
+                    bias=neg_max[:, c : c + 1], scale=1.0, accum_out=total[:, c : c + 1],
                 )
-                inverse = stats_pool.tile([P, 1], F32)
-                nc.vector.reciprocal(inverse[:], total[:])
-                nc.scalar.activation(out=probs[:, c, :], in_=probs[:, c, :], func=ACT.Copy, scale=inverse[:])
+            inverse = stats_pool.tile([P, UNIT_TILES], F32)
+            nc.vector.reciprocal(inverse[:], total[:])
+            for c in range(UNIT_TILES):
+                nc.scalar.activation(
+                    out=probs[:, c, :], in_=probs[:, c, :], func=ACT.Copy, scale=inverse[:, c : c + 1]
+                )
             return probs
 
         def store(probs, head, part):

@@ -26,12 +26,14 @@ HID = 512
 HALF = HID // 2
 TILES = NB // P
 P_BLOCKS = P // BS
+RUNS = (1, 2)
 MASKED = 1.0e9
 
 UNIT_TILES = 2
 UNIT_BLOCKS = UNIT_TILES * P
 UNIT_POSITIONS = UNIT_BLOCKS * BS
 UNITS = TILES // UNIT_TILES
+PAIRED_UNITS = 8
 LOADS_AHEAD = 3
 STORE_LAG = 8
 
@@ -60,7 +62,7 @@ def tile_attngate_e_kernel(
 
         ident = consts.tile([P, P], F32)
         ident_bf = consts.tile([P, P], BF16)
-        block_mean = consts.tile([P, P_BLOCKS], BF16)
+        block_mean = {run: consts.tile([P, P_BLOCKS * run], BF16, name=f"block_mean_{run}") for run in RUNS}
         w_words = consts.tile([P, HK + HQ, HID], I32, align_bytes=64)
         w_scales = consts.tile([P, HK + HQ, HID], U8, align_bytes=64)
         rope = consts.tile([P, TILES, 2, HID], BF16)
@@ -71,23 +73,28 @@ def tile_attngate_e_kernel(
 
         make_identity(nc, ident[:])
         make_identity(nc, ident_bf[:])
-        nc.gpsimd.memset(block_mean[:], 1.0 / BS)
-        nc.gpsimd.affine_select(
-            out=block_mean[:], in_=block_mean[:], compare_op=ALU.is_ge, fill=0.0,
-            base=0, pattern=[[-BS, P_BLOCKS]], channel_multiplier=1,
-        )
-        nc.gpsimd.affine_select(
-            out=block_mean[:], in_=block_mean[:], compare_op=ALU.is_ge, fill=0.0,
-            base=BS - 1, pattern=[[BS, P_BLOCKS]], channel_multiplier=-1,
-        )
+        for run in reversed(RUNS):
+            weights, span = block_mean[run], BS // run
+            nc.gpsimd.memset(weights[:], 1.0 / BS)
+            nc.gpsimd.affine_select(
+                out=weights[:], in_=weights[:], compare_op=ALU.is_ge, fill=0.0,
+                base=0, pattern=[[-span, P_BLOCKS * run]], channel_multiplier=1,
+            )
+            nc.gpsimd.affine_select(
+                out=weights[:], in_=weights[:], compare_op=ALU.is_ge, fill=0.0,
+                base=span - 1, pattern=[[span, P_BLOCKS * run]], channel_multiplier=-1,
+            )
         nc.vector.memset(w_scales[:].bitcast(I32), 0)
 
         heads = [k[0, kv] for kv in range(HK)] + [q[0, h] for h in range(HQ)]
 
-        def load_unit(head, part):
+        def load_unit(head, part, run):
             positions = heads[head][UNIT_POSITIONS * part : UNIT_POSITIONS * (part + 1), :]
             by_position = loads.tile([P, UNIT_POSITIONS // P, D], BF16)
-            nc.sync.dma_start(out=by_position[:], in_=positions.rearrange("(n p) d -> p n d", p=P))
+            nc.sync.dma_start(
+                out=by_position[:].rearrange("p (n e) d -> p n (e d)", e=run),
+                in_=positions.rearrange("(n p e) d -> p n (e d)", p=P, e=run),
+            )
             by_block = loads.tile([P, UNIT_TILES, BS * D], BF16)
             nc.sync.dma_start(
                 out=by_block[:], in_=positions.rearrange("(c p j) d -> p c (j d)", c=UNIT_TILES, p=P)
@@ -95,7 +102,7 @@ def tile_attngate_e_kernel(
             if part == 0:
                 words = wk_words[head] if head < HK else wq_words[head - HK]
                 nc.sync.dma_start(out=w_words[:, head, :], in_=words.rearrange("p n t -> p (n t)").bitcast(I32))
-            return by_position, by_block
+            return by_position, by_block, run
 
         def load_scales(first, count, scales):
             some = slice(first, first + count)
@@ -127,18 +134,20 @@ def tile_attngate_e_kernel(
                 op1=ALU.mult,
             )
 
-        def pool_unit(by_position, by_block):
+        def pool_unit(by_position, by_block, run):
             pooled = rows_pool.tile([P, UNIT_TILES, K], BF16)
             mean_t = mean_psum.tile([P, 2, UNIT_BLOCKS], F32)
-            for n in range(UNIT_POSITIONS // P):
+            width = P_BLOCKS * run
+            for n in range(UNIT_BLOCKS // width):
                 for f in range(2):
-                    nc.tensor.matmul(
-                        out=mean_t[:, f, P_BLOCKS * n : P_BLOCKS * (n + 1)],
-                        lhsT=by_position[:, n, P * f : P * (f + 1)],
-                        rhs=block_mean[:],
-                        start=True,
-                        stop=True,
-                    )
+                    for e in range(run):
+                        nc.tensor.matmul(
+                            out=mean_t[:, f, width * n : width * (n + 1)],
+                            lhsT=by_position[:, run * n + e, P * f : P * (f + 1)],
+                            rhs=block_mean[run][:],
+                            start=e == 0,
+                            stop=e == run - 1,
+                        )
             mean_bf = trees.tile([P, 2, UNIT_BLOCKS], BF16)
             nc.scalar.copy(out=mean_bf[:], in_=mean_t[:])
             mean_rows = flip_psum.tile([P, UNIT_TILES, D], BF16, tag="flip")
@@ -264,20 +273,21 @@ def tile_attngate_e_kernel(
                     units.append((head, part))
         n_units = len(units)
         loaded, pooled_mx, rotated_mx, finished = {}, {}, {}, {}
-        loaded[0] = load_unit(units[0][0], units[0][1])
+        runs = [2 if i < PAIRED_UNITS else 1 for i in range(n_units)]
+        loaded[0] = load_unit(units[0][0], units[0][1], runs[0])
         load_scales(0, HK, wk_scales)
         load_scales(HK, HQ, wq_scales)
         load_rope_tables()
-        loaded[1] = load_unit(units[1][0], units[1][1])
-        loaded[2] = load_unit(units[2][0], units[2][1])
+        loaded[1] = load_unit(units[1][0], units[1][1], runs[1])
+        loaded[2] = load_unit(units[2][0], units[2][1], runs[2])
         load_mask()
         for step in range(n_units + 2 + STORE_LAG):
             i = step + LOADS_AHEAD
             if i < n_units:
-                loaded[i] = load_unit(units[i][0], units[i][1])
+                loaded[i] = load_unit(units[i][0], units[i][1], runs[i])
             i = step
             if i < n_units:
-                pooled_mx[i] = quantise_pooled(pool_unit(loaded[i][0], loaded[i][1]))
+                pooled_mx[i] = quantise_pooled(pool_unit(loaded[i][0], loaded[i][1], loaded[i][2]))
             i = step - 1
             if 0 <= i < n_units:
                 head, part = units[i]

@@ -35,7 +35,7 @@ UNIT_POSITIONS = UNIT_BLOCKS * BS
 UNITS = TILES // UNIT_TILES
 PAIRED_UNITS = 8
 LOADS_AHEAD = 3
-STORE_LAG = 8
+STORE_LAG = 6
 
 FLOPS = 2 * (HQ + HK) * NB * K * HID + 2 * HQ * NB * NB * HID
 
@@ -47,18 +47,11 @@ def tile_attngate_e_kernel(
     with ExitStack() as ctx:
         consts = ctx.enter_context(tc.tile_pool(name="consts", bufs=1))
         loads = ctx.enter_context(tc.tile_pool(name="loads", bufs=LOADS_AHEAD + 1))
-        trees = ctx.enter_context(tc.tile_pool(name="trees", bufs=2))
-        rows_pool = ctx.enter_context(tc.tile_pool(name="rows", bufs=2))
-        grouped_pool = ctx.enter_context(tc.tile_pool(name="grouped", bufs=3))
-        codes_pool = ctx.enter_context(tc.tile_pool(name="codes", bufs=2))
-        rope_pool = ctx.enter_context(tc.tile_pool(name="rope", bufs=3))
-        soft_pool = ctx.enter_context(tc.tile_pool(name="soft", bufs=3))
+        work = ctx.enter_context(tc.tile_pool(name="work", bufs=2))
         probs_pool = ctx.enter_context(tc.tile_pool(name="probs", bufs=STORE_LAG + 2))
-        stats_pool = ctx.enter_context(tc.tile_pool(name="stats", bufs=4))
-        mean_psum = ctx.enter_context(tc.psum_pool(name="mean", bufs=2))
-        flip_psum = ctx.enter_context(tc.psum_pool(name="flip", bufs=2))
-        proj_psum = ctx.enter_context(tc.psum_pool(name="proj", bufs=2))
-        score_psum = ctx.enter_context(tc.psum_pool(name="score", bufs=2))
+        stats_pool = ctx.enter_context(tc.tile_pool(name="stats", bufs=3))
+        flip_psum = ctx.enter_context(tc.psum_pool(name="flip", bufs=1))
+        mx_psum = ctx.enter_context(tc.psum_pool(name="mx", bufs=2))
 
         ident = consts.tile([P, P], F32)
         ident_bf = consts.tile([P, P], BF16)
@@ -86,9 +79,19 @@ def tile_attngate_e_kernel(
             )
         nc.vector.memset(w_scales[:].bitcast(I32), 0)
 
+        units = []
+        for kv in range(HK):
+            for head in [kv] + [HK + GROUP * kv + g for g in range(GROUP)]:
+                for part in range(UNITS):
+                    units.append((head, part))
+        n_units = len(units)
+        runs = [2 if i < PAIRED_UNITS else 1 for i in range(n_units)]
+        state = [{} for i in range(n_units)]
         heads = [k[0, kv] for kv in range(HK)] + [q[0, h] for h in range(HQ)]
 
-        def load_unit(head, part, run):
+        def load_unit(i):
+            head, part = units[i]
+            run = runs[i]
             positions = heads[head][UNIT_POSITIONS * part : UNIT_POSITIONS * (part + 1), :]
             by_position = loads.tile([P, UNIT_POSITIONS // P, D], BF16)
             nc.sync.dma_start(
@@ -102,7 +105,7 @@ def tile_attngate_e_kernel(
             if part == 0:
                 words = wk_words[head] if head < HK else wq_words[head - HK]
                 nc.sync.dma_start(out=w_words[:, head, :], in_=words.rearrange("p n t -> p (n t)").bitcast(I32))
-            return by_position, by_block, run
+            state[i]["by_position"], state[i]["by_block"] = by_position, by_block
 
         def load_scales(first, count, scales):
             some = slice(first, first + count)
@@ -118,6 +121,8 @@ def tile_attngate_e_kernel(
             nc.sync.dma_start(out=rope[:, :, 0, :], in_=cos_rows)
             nc.sync.dma_start(out=rope[:, :, 1, 0:HALF], in_=sin_rows[:, :, HALF:])
             nc.sync.dma_start(out=rope[:, :, 1, HALF:], in_=sin_rows[:, :, 0:HALF])
+
+        def negate_rope_half():
             nc.vector.tensor_scalar_mul(rope[:, :, 1, HALF:], rope[:, :, 1, HALF:], -1.0)
 
         def load_mask():
@@ -125,6 +130,8 @@ def tile_attngate_e_kernel(
                 out=mask_words[:],
                 in_=attention_mask.bitcast(I32)[0, 0].rearrange("(c p) w -> p c w", p=P),
             )
+
+        def make_mask_bias():
             nc.vector.tensor_scalar(
                 out=mask_bias[:],
                 in0=mask_words[:].rearrange("p c (j w) -> p c j w", w=2)[:, :, :, 0],
@@ -134,176 +141,286 @@ def tile_attngate_e_kernel(
                 op1=ALU.mult,
             )
 
-        def pool_unit(by_position, by_block, run):
-            pooled = rows_pool.tile([P, UNIT_TILES, K], BF16)
-            mean_t = mean_psum.tile([P, 2, UNIT_BLOCKS], F32)
+        def sum_positions(i):
+            s, run = state[i], runs[i]
+            mean_t = flip_psum.tile([P, 2, UNIT_BLOCKS], F32)
             width = P_BLOCKS * run
             for n in range(UNIT_BLOCKS // width):
                 for f in range(2):
                     for e in range(run):
                         nc.tensor.matmul(
                             out=mean_t[:, f, width * n : width * (n + 1)],
-                            lhsT=by_position[:, run * n + e, P * f : P * (f + 1)],
+                            lhsT=s["by_position"][:, run * n + e, P * f : P * (f + 1)],
                             rhs=block_mean[run][:],
                             start=e == 0,
                             stop=e == run - 1,
                         )
-            mean_bf = trees.tile([P, 2, UNIT_BLOCKS], BF16)
-            nc.scalar.copy(out=mean_bf[:], in_=mean_t[:])
-            mean_rows = flip_psum.tile([P, UNIT_TILES, D], BF16, tag="flip")
+            s["mean_t"] = mean_t
+
+        def round_means(i):
+            mean_bf = work.tile([P, 2, UNIT_BLOCKS], BF16)
+            nc.scalar.copy(out=mean_bf[:], in_=state[i]["mean_t"][:])
+            state[i]["mean_bf"] = mean_bf
+
+        def flip_means(i):
+            mean_rows = flip_psum.tile([P, UNIT_TILES, D], BF16)
             for c in range(UNIT_TILES):
                 for f in range(2):
                     nc.tensor.transpose(
-                        mean_rows[:, c, P * f : P * (f + 1)], mean_bf[:, f, P * c : P * (c + 1)], ident_bf[:]
+                        mean_rows[:, c, P * f : P * (f + 1)],
+                        state[i]["mean_bf"][:, f, P * c : P * (c + 1)],
+                        ident_bf[:],
                     )
-            nc.scalar.copy(out=pooled[:, :, 0:D], in_=mean_rows[:])
-            max4 = trees.tile([P, UNIT_TILES, 4 * D], BF16)
+            state[i]["mean_rows"] = mean_rows
+
+        def new_pooled(i):
+            pooled = work.tile([P, UNIT_TILES, K], BF16)
+            state[i]["pooled"] = pooled
+
+        def place_means(i):
+            nc.scalar.copy(out=state[i]["pooled"][:, :, 0:D], in_=state[i]["mean_rows"][:])
+
+        def max_of_8(i):
+            max4 = work.tile([P, UNIT_TILES, 4 * D], BF16)
+            by_block = state[i]["by_block"]
             nc.vector.tensor_tensor(
                 out=max4[:], in0=by_block[:, :, 0 : 4 * D], in1=by_block[:, :, 4 * D :], op=ALU.max
             )
-            max2 = trees.tile([P, UNIT_TILES, 2 * D], BF16)
-            nc.vector.tensor_tensor(out=max2[:], in0=max4[:, :, 0 : 2 * D], in1=max4[:, :, 2 * D :], op=ALU.max)
-            nc.vector.tensor_tensor(out=pooled[:, :, D:], in0=max2[:, :, 0:D], in1=max2[:, :, D:], op=ALU.max)
-            return pooled
+            state[i]["max4"] = max4
 
-        def quantise_pooled(pooled):
-            grouped = grouped_pool.tile([P, UNIT_BLOCKS, PACK], BF16, align_bytes=64)
-            grouped_flat = grouped[:].rearrange("p b t -> p (b t)")
-            flipped = flip_psum.tile([P, UNIT_TILES, 2, P], F32, tag="flip")
+        def max_of_4(i):
+            max2 = work.tile([P, UNIT_TILES, 2 * D], BF16)
+            max4 = state[i]["max4"]
+            nc.vector.tensor_tensor(out=max2[:], in0=max4[:, :, 0 : 2 * D], in1=max4[:, :, 2 * D :], op=ALU.max)
+            state[i]["max2"] = max2
+
+        def max_of_2(i):
+            max2 = state[i]["max2"]
+            nc.vector.tensor_tensor(
+                out=state[i]["pooled"][:, :, D:], in0=max2[:, :, 0:D], in1=max2[:, :, D:], op=ALU.max
+            )
+
+        def flip_pooled(i):
+            flipped = flip_psum.tile([P, UNIT_TILES, 2, P], F32)
             for c in range(UNIT_TILES):
-                words = pooled[:, c, :].bitcast(F32)
+                words = state[i]["pooled"][:, c, :].bitcast(F32)
                 for u in range(2):
                     nc.tensor.transpose(flipped[:, c, u, :], words[:, u : K // 2 : 2], ident[:])
-            nc.scalar.copy(
-                out=grouped_flat.bitcast(F32).rearrange("p (c b u) -> p c b u", c=UNIT_TILES, u=2),
-                in_=flipped[:].rearrange("p c u b -> p c b u"),
-            )
-            p_codes = codes_pool.tile([P, UNIT_BLOCKS], U32, align_bytes=64)
-            p_scales = codes_pool.tile([P, UNIT_BLOCKS], U8, align_bytes=64)
-            nc.vector.quantize_mx(out=p_codes[:].bitcast(FP8X4), scales=p_scales[:], in_=grouped_flat)
-            return p_codes, p_scales
+            state[i]["flipped"] = flipped
 
-        def project_rotate_quantise(p_codes, p_scales, head, part, codes, scales):
-            grouped = grouped_pool.tile([P, UNIT_BLOCKS, PACK], BF16, align_bytes=64)
+        def group_pooled(i):
+            p_grouped = work.tile([P, UNIT_BLOCKS * PACK], BF16, align_bytes=64)
+            nc.scalar.copy(
+                out=p_grouped[:].bitcast(F32).rearrange("p (c b u) -> p c b u", c=UNIT_TILES, u=2),
+                in_=state[i]["flipped"][:].rearrange("p c u b -> p c b u"),
+            )
+            state[i]["p_grouped"] = p_grouped
+
+        def quantise_pooled(i):
+            p_codes = work.tile([P, UNIT_BLOCKS], U32, align_bytes=64)
+            p_scales = work.tile([P, UNIT_BLOCKS], U8, align_bytes=64)
+            nc.vector.quantize_mx(out=p_codes[:].bitcast(FP8X4), scales=p_scales[:], in_=state[i]["p_grouped"][:])
+            state[i]["p_codes"], state[i]["p_scales"] = p_codes, p_scales
+
+        def project(i):
+            head = units[i][0]
             for c in range(UNIT_TILES):
                 blocks = slice(P * c, P * (c + 1))
-                tile_in_head = UNIT_TILES * part + c
-                proj = proj_psum.tile([P, HID], F32)
+                proj = mx_psum.tile([P, HID], F32)
                 nc.tensor.matmul_mx(
                     out=proj[:],
-                    lhsT=p_codes[:, blocks].bitcast(FP8X4),
-                    lhsT_scale=p_scales[:, blocks],
+                    lhsT=state[i]["p_codes"][:, blocks].bitcast(FP8X4),
+                    lhsT_scale=state[i]["p_scales"][:, blocks],
                     rhs=w_words[:, head, :].bitcast(FP8X4),
                     rhs_scale=w_scales[:, head, :],
                     start=True,
                     stop=True,
                 )
-                products = rope_pool.tile([P, 2, HID], F32)
-                nc.vector.tensor_tensor(
-                    out=products[:],
-                    in0=proj[:].unsqueeze(1).to_broadcast([P, 2, HID]),
-                    in1=rope[:, tile_in_head, :, :],
-                    op=ALU.mult,
+                state[i]["proj", c] = proj
+
+        def rotate(i, c):
+            products = work.tile([P, 2, HID], F32)
+            nc.vector.tensor_tensor(
+                out=products[:],
+                in0=state[i]["proj", c][:].unsqueeze(1).to_broadcast([P, 2, HID]),
+                in1=rope[:, UNIT_TILES * units[i][1] + c, :, :],
+                op=ALU.mult,
+            )
+            state[i]["products", c] = products
+
+        def flip_rotated(i, c):
+            products = state[i]["products", c]
+            rotated_t = flip_psum.tile([P, PACK, P], F32)
+            for t in range(PACK):
+                swapped = (P * t + HALF) % HID
+                nc.tensor.matmul(
+                    out=rotated_t[:, t, :], lhsT=products[:, 0, P * t : P * (t + 1)], rhs=ident[:],
+                    is_transpose=True, start=True, stop=False,
                 )
-                rotated_t = flip_psum.tile([P, PACK, P], F32, tag="flip")
-                for t in range(PACK):
-                    cols = slice(P * t, P * (t + 1))
-                    swapped = (P * t + HALF) % HID
-                    nc.tensor.matmul(
-                        out=rotated_t[:, t, :], lhsT=products[:, 0, cols], rhs=ident[:],
-                        is_transpose=True, start=True, stop=False,
-                    )
-                    nc.tensor.matmul(
-                        out=rotated_t[:, t, :], lhsT=products[:, 1, swapped : swapped + P], rhs=ident[:],
-                        is_transpose=True, start=False, stop=True,
-                    )
-                nc.scalar.copy(out=grouped[:, blocks, :], in_=rotated_t[:].rearrange("p t b -> p b t"))
-            nc.vector.quantize_mx(
-                out=codes.bitcast(FP8X4), scales=scales, in_=grouped[:].rearrange("p b t -> p (b t)")
+                nc.tensor.matmul(
+                    out=rotated_t[:, t, :], lhsT=products[:, 1, swapped : swapped + P], rhs=ident[:],
+                    is_transpose=True, start=False, stop=True,
+                )
+            state[i]["rotated_t"] = rotated_t
+
+        def group_rotated(i, c):
+            if c == 0:
+                r_grouped = work.tile([P, UNIT_BLOCKS, PACK], BF16, align_bytes=64)
+                state[i]["r_grouped"] = r_grouped
+            nc.scalar.copy(
+                out=state[i]["r_grouped"][:, P * c : P * (c + 1), :],
+                in_=state[i]["rotated_t"][:].rearrange("p t b -> p b t"),
             )
 
-        def attend(q_codes, q_scales, head, part):
-            kv = (head - HK) // GROUP
-            probs = probs_pool.tile([P, UNIT_TILES, NB], F32)
-            masked = soft_pool.tile([P, UNIT_TILES, NB], F32)
+        def quantise_rotated(i):
+            head, part = units[i]
+            if head < HK:
+                some = slice(UNIT_BLOCKS * part, UNIT_BLOCKS * (part + 1))
+                codes, scales = k_codes[:, head, some], k_scales[:, head, some]
+            else:
+                q_codes = work.tile([P, UNIT_BLOCKS], U32, align_bytes=64)
+                q_scales = work.tile([P, UNIT_BLOCKS], U8, align_bytes=64)
+                codes, scales = q_codes[:], q_scales[:]
+                state[i]["q_codes"], state[i]["q_scales"] = q_codes, q_scales
+            nc.vector.quantize_mx(
+                out=codes.bitcast(FP8X4), scales=scales, in_=state[i]["r_grouped"][:].rearrange("p b t -> p (b t)")
+            )
+
+        def score(i):
+            kv = (units[i][0] - HK) // GROUP
             for c in range(UNIT_TILES):
                 blocks = slice(P * c, P * (c + 1))
-                score = score_psum.tile([P, NB], F32)
+                scores = mx_psum.tile([P, NB], F32)
                 nc.tensor.matmul_mx(
-                    out=score[:],
-                    lhsT=q_codes[:, blocks].bitcast(FP8X4),
-                    lhsT_scale=q_scales[:, blocks],
+                    out=scores[:],
+                    lhsT=state[i]["q_codes"][:, blocks].bitcast(FP8X4),
+                    lhsT_scale=state[i]["q_scales"][:, blocks],
                     rhs=k_codes[:, kv, :].bitcast(FP8X4),
                     rhs_scale=k_scales[:, kv, :],
                     start=True,
                     stop=True,
                 )
-                nc.vector.scalar_tensor_tensor(
-                    out=masked[:, c, :],
-                    in0=score[:],
-                    scalar=1.0 / math.sqrt(HID),
-                    in1=mask_bias[:, UNIT_TILES * part + c, :],
-                    op0=ALU.mult,
-                    op1=ALU.add,
-                )
-            neg_max = stats_pool.tile([P, UNIT_TILES], F32)
-            nc.vector.tensor_reduce(out=neg_max[:], in_=masked[:], axis=AXIS.X, op=ALU.max, negate=True)
+                state[i]["scores", c] = scores
+
+        def mask_scores(i, c):
+            if c == 0:
+                masked = work.tile([P, UNIT_TILES, NB], F32)
+                state[i]["masked"] = masked
+            nc.vector.scalar_tensor_tensor(
+                out=state[i]["masked"][:, c, :],
+                in0=state[i]["scores", c][:],
+                scalar=1.0 / math.sqrt(HID),
+                in1=mask_bias[:, UNIT_TILES * units[i][1] + c, :],
+                op0=ALU.mult,
+                op1=ALU.add,
+            )
+
+        def row_max(i, c):
+            if c == 0:
+                neg_max = stats_pool.tile([P, UNIT_TILES], F32)
+                state[i]["neg_max"] = neg_max
+            nc.vector.tensor_reduce(
+                out=state[i]["neg_max"][:, c : c + 1], in_=state[i]["masked"][:, c, :],
+                axis=AXIS.X, op=ALU.max, negate=True,
+            )
+
+        def exponentials(i):
+            probs = probs_pool.tile([P, UNIT_TILES, NB], F32)
             total = stats_pool.tile([P, UNIT_TILES], F32)
             for c in range(UNIT_TILES):
                 nc.scalar.activation(
-                    out=probs[:, c, :], in_=masked[:, c, :], func=ACT.Exp,
-                    bias=neg_max[:, c : c + 1], scale=1.0, accum_out=total[:, c : c + 1],
+                    out=probs[:, c, :], in_=state[i]["masked"][:, c, :], func=ACT.Exp,
+                    bias=state[i]["neg_max"][:, c : c + 1], scale=1.0, accum_out=total[:, c : c + 1],
                 )
+            state[i]["probs"], state[i]["total"] = probs, total
+
+        def invert(i):
             inverse = stats_pool.tile([P, UNIT_TILES], F32)
-            nc.vector.reciprocal(inverse[:], total[:])
+            nc.vector.reciprocal(inverse[:], state[i]["total"][:])
+            state[i]["inverse"] = inverse
+
+        def normalise(i):
+            probs = state[i]["probs"]
             for c in range(UNIT_TILES):
                 nc.scalar.activation(
-                    out=probs[:, c, :], in_=probs[:, c, :], func=ACT.Copy, scale=inverse[:, c : c + 1]
+                    out=probs[:, c, :], in_=probs[:, c, :], func=ACT.Copy, scale=state[i]["inverse"][:, c : c + 1]
                 )
-            return probs
 
-        def store(probs, head, part):
+        def store(i):
+            head, part = units[i]
             rows = out[0, head - HK, UNIT_BLOCKS * part : UNIT_BLOCKS * (part + 1), :]
-            nc.sync.dma_start(out=rows.rearrange("(c p) j -> p c j", p=P), in_=probs[:])
+            nc.sync.dma_start(out=rows.rearrange("(c p) j -> p c j", p=P), in_=state[i]["probs"][:])
 
-        units = []
-        for kv in range(HK):
-            for head in [kv] + [HK + GROUP * kv + g for g in range(GROUP)]:
-                for part in range(UNITS):
-                    units.append((head, part))
-        n_units = len(units)
-        loaded, pooled_mx, rotated_mx, finished = {}, {}, {}, {}
-        runs = [2 if i < PAIRED_UNITS else 1 for i in range(n_units)]
-        loaded[0] = load_unit(units[0][0], units[0][1], runs[0])
+        def unit_at(i):
+            return 0 <= i < n_units
+
+        def query_at(i):
+            return 0 <= i < n_units and units[i][0] >= HK
+
+        ctx.enter_context(tc.manual_schedule())
+        load_unit(0)
         load_scales(0, HK, wk_scales)
         load_scales(HK, HQ, wq_scales)
         load_rope_tables()
-        loaded[1] = load_unit(units[1][0], units[1][1], runs[1])
-        loaded[2] = load_unit(units[2][0], units[2][1], runs[2])
+        load_unit(1)
+        load_unit(2)
         load_mask()
-        for step in range(n_units + 2 + STORE_LAG):
-            i = step + LOADS_AHEAD
-            if i < n_units:
-                loaded[i] = load_unit(units[i][0], units[i][1], runs[i])
-            i = step
-            if i < n_units:
-                pooled_mx[i] = quantise_pooled(pool_unit(loaded[i][0], loaded[i][1], loaded[i][2]))
-            i = step - 1
-            if 0 <= i < n_units:
-                head, part = units[i]
-                if head < HK:
-                    some = slice(UNIT_BLOCKS * part, UNIT_BLOCKS * (part + 1))
-                    project_rotate_quantise(
-                        pooled_mx[i][0], pooled_mx[i][1], head, part, k_codes[:, head, some], k_scales[:, head, some]
-                    )
-                else:
-                    q_codes = codes_pool.tile([P, UNIT_BLOCKS], U32, align_bytes=64)
-                    q_scales = codes_pool.tile([P, UNIT_BLOCKS], U8, align_bytes=64)
-                    project_rotate_quantise(pooled_mx[i][0], pooled_mx[i][1], head, part, q_codes[:], q_scales[:])
-                    rotated_mx[i] = (q_codes, q_scales)
-            i = step - 2
-            if 0 <= i < n_units and units[i][0] >= HK:
-                finished[i] = attend(rotated_mx[i][0], rotated_mx[i][1], units[i][0], units[i][1])
-            i = step - 2 - STORE_LAG
-            if 0 <= i < n_units and units[i][0] >= HK:
-                store(finished[i], units[i][0], units[i][1])
+        for i in range(n_units + 4 + STORE_LAG):
+            if unit_at(i + LOADS_AHEAD):
+                load_unit(i + LOADS_AHEAD)
+            if query_at(i - 4 - STORE_LAG):
+                store(i - 4 - STORE_LAG)
+            if unit_at(i):
+                new_pooled(i)
+            if unit_at(i - 1):
+                flip_pooled(i - 1)
+            if query_at(i - 4):
+                exponentials(i - 4)
+            if unit_at(i - 2):
+                rotate(i - 2, 0)
+            if unit_at(i - 1):
+                group_pooled(i - 1)
+            if unit_at(i - 2):
+                flip_rotated(i - 2, 0)
+            if unit_at(i):
+                max_of_8(i)
+            if unit_at(i - 2):
+                group_rotated(i - 2, 0)
+                rotate(i - 2, 1)
+            if unit_at(i):
+                sum_positions(i)
+            if query_at(i - 4):
+                invert(i - 4)
+            if unit_at(i):
+                round_means(i)
+            if unit_at(i - 2):
+                flip_rotated(i - 2, 1)
+            if unit_at(i):
+                max_of_4(i)
+            if query_at(i - 4):
+                normalise(i - 4)
+            if query_at(i - 3):
+                mask_scores(i - 3, 0)
+            if unit_at(i - 2):
+                group_rotated(i - 2, 1)
+            if unit_at(i):
+                max_of_2(i)
+                flip_means(i)
+                place_means(i)
+            if query_at(i - 3):
+                mask_scores(i - 3, 1)
+            if i == 1:
+                negate_rope_half()
+            if i == 3:
+                make_mask_bias()
+            if unit_at(i - 1):
+                quantise_pooled(i - 1)
+                project(i - 1)
+            if query_at(i - 3):
+                row_max(i - 3, 0)
+            if unit_at(i - 2):
+                quantise_rotated(i - 2)
+            if query_at(i - 2):
+                score(i - 2)
+            if query_at(i - 3):
+                row_max(i - 3, 1)

@@ -30,10 +30,13 @@ RUNS = (1, 2)
 MASKED = 1.0e9
 
 UNIT_TILES = 2
+WHOLE = [slice(0, UNIT_TILES)]
+TILE_BY_TILE = [slice(c, c + 1) for c in range(UNIT_TILES)]
 UNIT_BLOCKS = UNIT_TILES * P
 UNIT_POSITIONS = UNIT_BLOCKS * BS
 UNITS = TILES // UNIT_TILES
-PAIRED_UNITS = 8
+SUMMED_UNITS = 4
+PAIRED_UNITS = 12
 LOADS_AHEAD = 3
 STORE_LAG = 6
 
@@ -48,6 +51,7 @@ def tile_attngate_e_kernel(
         consts = ctx.enter_context(tc.tile_pool(name="consts", bufs=1))
         loads = ctx.enter_context(tc.tile_pool(name="loads", bufs=LOADS_AHEAD + 1))
         work = ctx.enter_context(tc.tile_pool(name="work", bufs=2))
+        sums_pool = ctx.enter_context(tc.tile_pool(name="sums", bufs=1))
         probs_pool = ctx.enter_context(tc.tile_pool(name="probs", bufs=STORE_LAG + 2))
         stats_pool = ctx.enter_context(tc.tile_pool(name="stats", bufs=3))
         flip_psum = ctx.enter_context(tc.psum_pool(name="flip", bufs=1))
@@ -85,7 +89,7 @@ def tile_attngate_e_kernel(
                 for part in range(UNITS):
                     units.append((head, part))
         n_units = len(units)
-        runs = [2 if i < PAIRED_UNITS else 1 for i in range(n_units)]
+        runs = [None] * SUMMED_UNITS + [2] * PAIRED_UNITS + [1] * (n_units - SUMMED_UNITS - PAIRED_UNITS)
         state = [{} for i in range(n_units)]
         heads = [k[0, kv] for kv in range(HK)] + [q[0, h] for h in range(HQ)]
 
@@ -93,19 +97,21 @@ def tile_attngate_e_kernel(
             head, part = units[i]
             run = runs[i]
             positions = heads[head][UNIT_POSITIONS * part : UNIT_POSITIONS * (part + 1), :]
-            by_position = loads.tile([P, UNIT_POSITIONS // P, D], BF16)
-            nc.sync.dma_start(
-                out=by_position[:].rearrange("p (n e) d -> p n (e d)", e=run),
-                in_=positions.rearrange("(n p e) d -> p n (e d)", p=P, e=run),
-            )
+            if run is not None:
+                by_position = loads.tile([P, UNIT_POSITIONS // P, D], BF16)
+                nc.sync.dma_start(
+                    out=by_position[:].rearrange("p (n e) d -> p n (e d)", e=run),
+                    in_=positions.rearrange("(n p e) d -> p n (e d)", p=P, e=run),
+                )
+                state[i]["by_position"] = by_position
             by_block = loads.tile([P, UNIT_TILES, BS * D], BF16)
-            nc.sync.dma_start(
-                out=by_block[:], in_=positions.rearrange("(c p j) d -> p c (j d)", c=UNIT_TILES, p=P)
-            )
+            rows = positions.rearrange("(c p j) d -> p c (j d)", c=UNIT_TILES, p=P)
+            for some in WHOLE if run is not None else TILE_BY_TILE:
+                nc.sync.dma_start(out=by_block[:, some, :], in_=rows[:, some, :])
+            state[i]["by_block"] = by_block
             if part == 0:
                 words = wk_words[head] if head < HK else wq_words[head - HK]
                 nc.sync.dma_start(out=w_words[:, head, :], in_=words.rearrange("p n t -> p (n t)").bitcast(I32))
-            state[i]["by_position"], state[i]["by_block"] = by_position, by_block
 
         def load_scales(first, count, scales):
             some = slice(first, first + count)
@@ -125,20 +131,21 @@ def tile_attngate_e_kernel(
         def negate_rope_half():
             nc.vector.tensor_scalar_mul(rope[:, :, 1, HALF:], rope[:, :, 1, HALF:], -1.0)
 
-        def load_mask():
+        def load_mask(part):
+            some = slice(UNIT_TILES * part, UNIT_TILES * (part + 1))
             nc.sync.dma_start(
-                out=mask_words[:],
-                in_=attention_mask.bitcast(I32)[0, 0].rearrange("(c p) w -> p c w", p=P),
+                out=mask_words[:, some, :],
+                in_=attention_mask.bitcast(I32)[0, 0].rearrange("(c p) w -> p c w", p=P)[:, some, :],
             )
 
-        def make_mask_bias():
-            nc.vector.tensor_scalar(
-                out=mask_bias[:],
-                in0=mask_words[:].rearrange("p c (j w) -> p c j w", w=2)[:, :, :, 0],
-                scalar1=1.0,
-                scalar2=MASKED,
-                op0=ALU.subtract,
-                op1=ALU.mult,
+        def make_mask_bias(part):
+            some = slice(UNIT_TILES * part, UNIT_TILES * (part + 1))
+            nc.scalar.activation(
+                out=mask_bias[:, some, :],
+                in_=mask_words[:, some, :].bitcast(U32).rearrange("p c (j w) -> p c j w", w=2)[:, :, :, 0],
+                func=ACT.Copy,
+                scale=MASKED,
+                bias=-MASKED,
             )
 
         def sum_positions(i):
@@ -157,9 +164,35 @@ def tile_attngate_e_kernel(
                         )
             s["mean_t"] = mean_t
 
+        def pair_positions(i):
+            for c in range(UNIT_TILES):
+                by_block = state[i]["by_block"]
+                pairs = sums_pool.tile([P, BS // 2, D], F32, tag=f"pairs_{c}")
+                nc.vector.tensor_tensor(
+                    out=pairs[:].rearrange("p j d -> p (j d)"),
+                    in0=by_block[:, c, 0 : 4 * D], in1=by_block[:, c, 4 * D :], op=ALU.add,
+                )
+                state[i]["pairs", c] = pairs
+
+        def sum_pairs(i):
+            mean_t = flip_psum.tile([P, 2, UNIT_BLOCKS], F32)
+            for c in range(UNIT_TILES):
+                for f in range(2):
+                    for j in range(BS // 2):
+                        nc.tensor.matmul(
+                            out=mean_t[:, f, P * c : P * (c + 1)],
+                            lhsT=state[i]["pairs", c][:, j, P * f : P * (f + 1)],
+                            rhs=ident[:],
+                            is_transpose=True, start=j == 0, stop=j == BS // 2 - 1,
+                        )
+            state[i]["mean_t"] = mean_t
+
         def round_means(i):
             mean_bf = work.tile([P, 2, UNIT_BLOCKS], BF16)
-            nc.scalar.copy(out=mean_bf[:], in_=state[i]["mean_t"][:])
+            if runs[i] is None:
+                nc.scalar.activation(out=mean_bf[:], in_=state[i]["mean_t"][:], func=ACT.Copy, scale=1.0 / BS)
+            else:
+                nc.scalar.copy(out=mean_bf[:], in_=state[i]["mean_t"][:])
             state[i]["mean_bf"] = mean_bf
 
         def flip_means(i):
@@ -183,9 +216,10 @@ def tile_attngate_e_kernel(
         def max_of_8(i):
             max4 = work.tile([P, UNIT_TILES, 4 * D], BF16)
             by_block = state[i]["by_block"]
-            nc.vector.tensor_tensor(
-                out=max4[:], in0=by_block[:, :, 0 : 4 * D], in1=by_block[:, :, 4 * D :], op=ALU.max
-            )
+            for some in WHOLE if runs[i] is not None else TILE_BY_TILE:
+                nc.vector.tensor_tensor(
+                    out=max4[:, some, :], in0=by_block[:, some, 0 : 4 * D], in1=by_block[:, some, 4 * D :], op=ALU.max
+                )
             state[i]["max4"] = max4
 
         def max_of_4(i):
@@ -222,21 +256,20 @@ def tile_attngate_e_kernel(
             nc.vector.quantize_mx(out=p_codes[:].bitcast(FP8X4), scales=p_scales[:], in_=state[i]["p_grouped"][:])
             state[i]["p_codes"], state[i]["p_scales"] = p_codes, p_scales
 
-        def project(i):
+        def project(i, c):
             head = units[i][0]
-            for c in range(UNIT_TILES):
-                blocks = slice(P * c, P * (c + 1))
-                proj = mx_psum.tile([P, HID], F32)
-                nc.tensor.matmul_mx(
-                    out=proj[:],
-                    lhsT=state[i]["p_codes"][:, blocks].bitcast(FP8X4),
-                    lhsT_scale=state[i]["p_scales"][:, blocks],
-                    rhs=w_words[:, head, :].bitcast(FP8X4),
-                    rhs_scale=w_scales[:, head, :],
-                    start=True,
-                    stop=True,
-                )
-                state[i]["proj", c] = proj
+            blocks = slice(P * c, P * (c + 1))
+            proj = mx_psum.tile([P, HID], F32)
+            nc.tensor.matmul_mx(
+                out=proj[:],
+                lhsT=state[i]["p_codes"][:, blocks].bitcast(FP8X4),
+                lhsT_scale=state[i]["p_scales"][:, blocks],
+                rhs=w_words[:, head, :].bitcast(FP8X4),
+                rhs_scale=w_scales[:, head, :],
+                start=True,
+                stop=True,
+            )
+            state[i]["proj", c] = proj
 
         def rotate(i, c):
             products = work.tile([P, 2, HID], F32)
@@ -349,7 +382,10 @@ def tile_attngate_e_kernel(
         def store(i):
             head, part = units[i]
             rows = out[0, head - HK, UNIT_BLOCKS * part : UNIT_BLOCKS * (part + 1), :]
-            nc.sync.dma_start(out=rows.rearrange("(c p) j -> p c j", p=P), in_=state[i]["probs"][:])
+            for some in TILE_BY_TILE if i == n_units - 1 else WHOLE:
+                nc.sync.dma_start(
+                    out=rows.rearrange("(c p) j -> p c j", p=P)[:, some, :], in_=state[i]["probs"][:, some, :]
+                )
 
         def unit_at(i):
             return 0 <= i < n_units
@@ -360,67 +396,72 @@ def tile_attngate_e_kernel(
         ctx.enter_context(tc.manual_schedule())
         load_unit(0)
         load_scales(0, HK, wk_scales)
-        load_scales(HK, HQ, wq_scales)
         load_rope_tables()
         load_unit(1)
         load_unit(2)
-        load_mask()
+        load_scales(HK, HQ, wq_scales)
         for i in range(n_units + 4 + STORE_LAG):
+            new, old, turn, last, end = unit_at(i), unit_at(i - 1), unit_at(i - 2), unit_at(i - 3), query_at(i - 4)
+            attend = query_at(i - 3)
             if unit_at(i + LOADS_AHEAD):
                 load_unit(i + LOADS_AHEAD)
+            if i < UNITS:
+                load_mask(i)
             if query_at(i - 4 - STORE_LAG):
                 store(i - 4 - STORE_LAG)
-            if unit_at(i):
-                new_pooled(i)
-            if unit_at(i - 1):
-                flip_pooled(i - 1)
-            if query_at(i - 4):
+            if end:
                 exponentials(i - 4)
-            if unit_at(i - 2):
+            if turn:
                 rotate(i - 2, 0)
-            if unit_at(i - 1):
-                group_pooled(i - 1)
-            if unit_at(i - 2):
+            if last:
+                quantise_rotated(i - 3)
+            if turn:
                 flip_rotated(i - 2, 0)
-            if unit_at(i):
-                max_of_8(i)
-            if unit_at(i - 2):
+            if attend:
+                score(i - 3)
+            if turn:
                 group_rotated(i - 2, 0)
+            if new:
+                if runs[i] is None:
+                    pair_positions(i)
+                new_pooled(i)
+                max_of_8(i)
+                if runs[i] is None:
+                    sum_pairs(i)
+                else:
+                    sum_positions(i)
+            if turn:
                 rotate(i - 2, 1)
-            if unit_at(i):
-                sum_positions(i)
-            if query_at(i - 4):
+            if end:
                 invert(i - 4)
-            if unit_at(i):
-                round_means(i)
-            if unit_at(i - 2):
-                flip_rotated(i - 2, 1)
-            if unit_at(i):
-                max_of_4(i)
-            if query_at(i - 4):
                 normalise(i - 4)
-            if query_at(i - 3):
-                mask_scores(i - 3, 0)
-            if unit_at(i - 2):
+            if old:
+                quantise_pooled(i - 1)
+            if new:
+                round_means(i)
+                max_of_4(i)
+            if turn:
+                flip_rotated(i - 2, 1)
+            if old:
+                for c in range(UNIT_TILES):
+                    project(i - 1, c)
+            if turn:
                 group_rotated(i - 2, 1)
-            if unit_at(i):
+            if attend:
+                mask_scores(i - 3, 0)
+            if new:
                 max_of_2(i)
                 flip_means(i)
                 place_means(i)
-            if query_at(i - 3):
+            if attend:
                 mask_scores(i - 3, 1)
             if i == 1:
                 negate_rope_half()
-            if i == 3:
-                make_mask_bias()
-            if unit_at(i - 1):
-                quantise_pooled(i - 1)
-                project(i - 1)
-            if query_at(i - 3):
-                row_max(i - 3, 0)
-            if unit_at(i - 2):
-                quantise_rotated(i - 2)
-            if query_at(i - 2):
-                score(i - 2)
-            if query_at(i - 3):
-                row_max(i - 3, 1)
+            if i in (3, 4):
+                make_mask_bias(i - 3)
+            if new:
+                flip_pooled(i)
+                group_pooled(i)
+            if attend:
+                for c in range(UNIT_TILES):
+                    row_max(i - 3, c)

@@ -348,14 +348,12 @@ def tile_attngate_e_kernel(
                 op1=ALU.add,
             )
 
-        def row_max(i, c):
-            if c == 0:
-                neg_max = stats_pool.tile([P, UNIT_TILES], F32)
-                state[i]["neg_max"] = neg_max
+        def row_max(i):
+            neg_max = stats_pool.tile([P, UNIT_TILES], F32)
             nc.vector.tensor_reduce(
-                out=state[i]["neg_max"][:, c : c + 1], in_=state[i]["masked"][:, c, :],
-                axis=AXIS.X, op=ALU.max, negate=True,
+                out=neg_max[:], in_=state[i]["masked"][:], axis=AXIS.X, op=ALU.max, negate=True
             )
+            state[i]["neg_max"] = neg_max
 
         def exponentials(i):
             probs = probs_pool.tile([P, UNIT_TILES, NB], F32)
@@ -396,8 +394,8 @@ def tile_attngate_e_kernel(
         ctx.enter_context(tc.manual_schedule())
         load_unit(0)
         load_scales(0, HK, wk_scales)
-        load_rope_tables()
         load_unit(1)
+        load_rope_tables()
         load_unit(2)
         load_scales(HK, HQ, wq_scales)
         for i in range(n_units + 4 + STORE_LAG):
@@ -405,8 +403,8 @@ def tile_attngate_e_kernel(
             attend = query_at(i - 3)
             if unit_at(i + LOADS_AHEAD):
                 load_unit(i + LOADS_AHEAD)
-            if i < UNITS:
-                load_mask(i)
+            if i in (0, 2):
+                load_mask(i // 2)
             if query_at(i - 4 - STORE_LAG):
                 store(i - 4 - STORE_LAG)
             if end:
@@ -449,19 +447,17 @@ def tile_attngate_e_kernel(
                 group_rotated(i - 2, 1)
             if attend:
                 mask_scores(i - 3, 0)
+                mask_scores(i - 3, 1)
             if new:
                 max_of_2(i)
                 flip_means(i)
                 place_means(i)
-            if attend:
-                mask_scores(i - 3, 1)
             if i == 1:
                 negate_rope_half()
-            if i in (3, 4):
-                make_mask_bias(i - 3)
+            if i in (4, 5):
+                make_mask_bias(i - 4)
             if new:
                 flip_pooled(i)
                 group_pooled(i)
             if attend:
-                for c in range(UNIT_TILES):
-                    row_max(i - 3, c)
+                row_max(i - 3)

@@ -53,7 +53,7 @@ def tile_attngate_e_kernel(
         work = ctx.enter_context(tc.tile_pool(name="work", bufs=2))
         sums_pool = ctx.enter_context(tc.tile_pool(name="sums", bufs=1))
         probs_pool = ctx.enter_context(tc.tile_pool(name="probs", bufs=STORE_LAG + 2))
-        stats_pool = ctx.enter_context(tc.tile_pool(name="stats", bufs=3))
+        stats_pool = ctx.enter_context(tc.tile_pool(name="stats", bufs=6))
         flip_psum = ctx.enter_context(tc.psum_pool(name="flip", bufs=1))
         mx_psum = ctx.enter_context(tc.psum_pool(name="mx", bufs=2))
 
@@ -305,29 +305,33 @@ def tile_attngate_e_kernel(
                 in_=state[i]["rotated_t"][:].rearrange("p t b -> p b t"),
             )
 
-        def quantise_rotated(i):
+        def new_codes(i):
             head, part = units[i]
             if head < HK:
                 some = slice(UNIT_BLOCKS * part, UNIT_BLOCKS * (part + 1))
-                codes, scales = k_codes[:, head, some], k_scales[:, head, some]
+                state[i]["codes"], state[i]["scales"] = k_codes[:, head, some], k_scales[:, head, some]
             else:
                 q_codes = work.tile([P, UNIT_BLOCKS], U32, align_bytes=64)
                 q_scales = work.tile([P, UNIT_BLOCKS], U8, align_bytes=64)
-                codes, scales = q_codes[:], q_scales[:]
-                state[i]["q_codes"], state[i]["q_scales"] = q_codes, q_scales
+                state[i]["codes"], state[i]["scales"] = q_codes[:], q_scales[:]
+
+        def quantise_rotated(i, some):
+            blocks = slice(P * some.start, P * some.stop)
             nc.vector.quantize_mx(
-                out=codes.bitcast(FP8X4), scales=scales, in_=state[i]["r_grouped"][:].rearrange("p b t -> p (b t)")
+                out=state[i]["codes"][:, blocks].bitcast(FP8X4),
+                scales=state[i]["scales"][:, blocks],
+                in_=state[i]["r_grouped"][:, blocks, :].rearrange("p b t -> p (b t)"),
             )
 
-        def score(i):
+        def score(i, some):
             kv = (units[i][0] - HK) // GROUP
-            for c in range(UNIT_TILES):
+            for c in range(some.start, some.stop):
                 blocks = slice(P * c, P * (c + 1))
                 scores = mx_psum.tile([P, NB], F32)
                 nc.tensor.matmul_mx(
                     out=scores[:],
-                    lhsT=state[i]["q_codes"][:, blocks].bitcast(FP8X4),
-                    lhsT_scale=state[i]["q_scales"][:, blocks],
+                    lhsT=state[i]["codes"][:, blocks].bitcast(FP8X4),
+                    lhsT_scale=state[i]["scales"][:, blocks],
                     rhs=k_codes[:, kv, :].bitcast(FP8X4),
                     rhs_scale=k_scales[:, kv, :],
                     start=True,
@@ -336,11 +340,10 @@ def tile_attngate_e_kernel(
                 state[i]["scores", c] = scores
 
         def mask_scores(i, c):
-            if c == 0:
-                masked = work.tile([P, UNIT_TILES, NB], F32)
-                state[i]["masked"] = masked
+            masked = work.tile([P, NB], F32, tag=f"masked_{c}")
+            state[i]["masked", c] = masked
             nc.vector.scalar_tensor_tensor(
-                out=state[i]["masked"][:, c, :],
+                out=masked[:],
                 in0=state[i]["scores", c][:],
                 scalar=1.0 / math.sqrt(HID),
                 in1=mask_bias[:, UNIT_TILES * units[i][1] + c, :],
@@ -348,20 +351,20 @@ def tile_attngate_e_kernel(
                 op1=ALU.add,
             )
 
-        def row_max(i):
-            neg_max = stats_pool.tile([P, UNIT_TILES], F32)
+        def row_max(i, c):
+            neg_max = stats_pool.tile([P, 1], F32)
             nc.vector.tensor_reduce(
-                out=neg_max[:], in_=state[i]["masked"][:], axis=AXIS.X, op=ALU.max, negate=True
+                out=neg_max[:], in_=state[i]["masked", c][:], axis=AXIS.X, op=ALU.max, negate=True
             )
-            state[i]["neg_max"] = neg_max
+            state[i]["neg_max", c] = neg_max
 
         def exponentials(i):
             probs = probs_pool.tile([P, UNIT_TILES, NB], F32)
             total = stats_pool.tile([P, UNIT_TILES], F32)
             for c in range(UNIT_TILES):
                 nc.scalar.activation(
-                    out=probs[:, c, :], in_=state[i]["masked"][:, c, :], func=ACT.Exp,
-                    bias=state[i]["neg_max"][:, c : c + 1], scale=1.0, accum_out=total[:, c : c + 1],
+                    out=probs[:, c, :], in_=state[i]["masked", c][:], func=ACT.Exp,
+                    bias=state[i]["neg_max", c][:], scale=1.0, accum_out=total[:, c : c + 1],
                 )
             state[i]["probs"], state[i]["total"] = probs, total
 
@@ -370,12 +373,13 @@ def tile_attngate_e_kernel(
             nc.vector.reciprocal(inverse[:], state[i]["total"][:])
             state[i]["inverse"] = inverse
 
-        def normalise(i):
-            probs = state[i]["probs"]
-            for c in range(UNIT_TILES):
-                nc.scalar.activation(
-                    out=probs[:, c, :], in_=probs[:, c, :], func=ACT.Copy, scale=state[i]["inverse"][:, c : c + 1]
-                )
+        def normalise(i, c):
+            rows = state[i]["probs"][:, c, :]
+            nc.scalar.activation(out=rows, in_=rows, func=ACT.Copy, scale=state[i]["inverse"][:, c : c + 1])
+
+        def normalise_on_vector(i, c):
+            rows = state[i]["probs"][:, c, :]
+            nc.vector.tensor_scalar_mul(rows, rows, state[i]["inverse"][:, c : c + 1])
 
         def store(i):
             head, part = units[i]
@@ -401,6 +405,7 @@ def tile_attngate_e_kernel(
         for i in range(n_units + 4 + STORE_LAG):
             new, old, turn, last, end = unit_at(i), unit_at(i - 1), unit_at(i - 2), unit_at(i - 3), query_at(i - 4)
             attend = query_at(i - 3)
+            drain = i >= n_units + 2
             if unit_at(i + LOADS_AHEAD):
                 load_unit(i + LOADS_AHEAD)
             if i in (0, 2):
@@ -411,12 +416,13 @@ def tile_attngate_e_kernel(
                 exponentials(i - 4)
             if turn:
                 rotate(i - 2, 0)
-            if last:
-                quantise_rotated(i - 3)
+            if last and not drain:
+                new_codes(i - 3)
+                quantise_rotated(i - 3, WHOLE[0])
             if turn:
                 flip_rotated(i - 2, 0)
-            if attend:
-                score(i - 3)
+            if attend and not drain:
+                score(i - 3, WHOLE[0])
             if turn:
                 group_rotated(i - 2, 0)
             if new:
@@ -430,9 +436,10 @@ def tile_attngate_e_kernel(
                     sum_positions(i)
             if turn:
                 rotate(i - 2, 1)
-            if end:
+            if end and not drain:
                 invert(i - 4)
-                normalise(i - 4)
+                for c in range(UNIT_TILES):
+                    normalise(i - 4, c)
             if old:
                 quantise_pooled(i - 1)
             if new:
@@ -445,13 +452,14 @@ def tile_attngate_e_kernel(
                     project(i - 1, c)
             if turn:
                 group_rotated(i - 2, 1)
-            if attend:
+            if attend and not drain:
                 mask_scores(i - 3, 0)
-                mask_scores(i - 3, 1)
             if new:
                 max_of_2(i)
                 flip_means(i)
                 place_means(i)
+            if attend and not drain:
+                mask_scores(i - 3, 1)
             if i == 1:
                 negate_rope_half()
             if i in (4, 5):
@@ -459,5 +467,25 @@ def tile_attngate_e_kernel(
             if new:
                 flip_pooled(i)
                 group_pooled(i)
-            if attend:
-                row_max(i - 3)
+            if i == n_units + 1:
+                new_codes(i - 2)
+                row_max(i - 3, 0)
+                quantise_rotated(i - 2, TILE_BY_TILE[0])
+                score(i - 2, TILE_BY_TILE[0])
+                row_max(i - 3, 1)
+                mask_scores(i - 2, 0)
+                quantise_rotated(i - 2, TILE_BY_TILE[1])
+                score(i - 2, TILE_BY_TILE[1])
+                row_max(i - 2, 0)
+                mask_scores(i - 2, 1)
+                row_max(i - 2, 1)
+            elif attend and not drain:
+                for c in range(UNIT_TILES):
+                    row_max(i - 3, c)
+            if end and drain:
+                invert(i - 4)
+                for c in range(UNIT_TILES):
+                    if c == 0 and i - 4 == n_units - 1:
+                        normalise(i - 4, c)
+                    else:
+                        normalise_on_vector(i - 4, c)

import math
from contextlib import ExitStack

import concourse.mybir as mybir
from concourse.masks import make_identity

FP8X4 = mybir.dt.float8_e4m3fn_x4
BF16 = mybir.dt.bfloat16
F32 = mybir.dt.float32
I32 = mybir.dt.int32
U32 = mybir.dt.uint32
U8 = mybir.dt.uint8
ALU = mybir.AluOpType
ACT = mybir.ActivationFunctionType
AXIS = mybir.AxisListType

P = 128
PACK = 4
HQ, HK = 8, 2
GROUP = HQ // HK
S, D = 4096, 256
BS = 8
NB = S // BS
K = 2 * D
HID = 512
HALF = HID // 2
TILES = NB // P
P_BLOCKS = P // BS
RUNS = (1, 2)
MASKED = 1.0e9

UNIT_TILES = 2
WHOLE = [slice(0, UNIT_TILES)]
TILE_BY_TILE = [slice(c, c + 1) for c in range(UNIT_TILES)]
UNIT_BLOCKS = UNIT_TILES * P
UNIT_POSITIONS = UNIT_BLOCKS * BS
UNITS = TILES // UNIT_TILES
SUMMED_UNITS = 4
PAIRED_UNITS = 12
LOADS_AHEAD = 3
STORE_LAG = 6

FLOPS = 2 * (HQ + HK) * NB * K * HID + 2 * HQ * NB * NB * HID


def tile_attngate_e_kernel(
    tc, q, k, attention_mask, cos, sin, wq_words, wq_scales, wk_words, wk_scales, out
):
    nc = tc.nc
    with ExitStack() as ctx:
        consts = ctx.enter_context(tc.tile_pool(name="consts", bufs=1))
        loads = ctx.enter_context(tc.tile_pool(name="loads", bufs=LOADS_AHEAD + 1))
        work = ctx.enter_context(tc.tile_pool(name="work", bufs=2))
        sums_pool = ctx.enter_context(tc.tile_pool(name="sums", bufs=1))
        probs_pool = ctx.enter_context(tc.tile_pool(name="probs", bufs=STORE_LAG + 2))
        stats_pool = ctx.enter_context(tc.tile_pool(name="stats", bufs=6))
        flip_psum = ctx.enter_context(tc.psum_pool(name="flip", bufs=1))
        mx_psum = ctx.enter_context(tc.psum_pool(name="mx", bufs=2))

        ident = consts.tile([P, P], F32)
        ident_bf = consts.tile([P, P], BF16)
        block_mean = {run: consts.tile([P, P_BLOCKS * run], BF16, name=f"block_mean_{run}") for run in RUNS}
        w_words = consts.tile([P, HK + HQ, HID], I32, align_bytes=64)
        w_scales = consts.tile([P, HK + HQ, HID], U8, align_bytes=64)
        rope = consts.tile([P, TILES, 2, HID], BF16)
        mask_words = consts.tile([P, TILES, 2 * NB], I32)
        mask_bias = consts.tile([P, TILES, NB], F32)
        k_codes = consts.tile([P, HK, NB], U32, align_bytes=64)
        k_scales = consts.tile([P, HK, NB], U8, align_bytes=64)

        make_identity(nc, ident[:])
        make_identity(nc, ident_bf[:])
        for run in reversed(RUNS):
            weights, span = block_mean[run], BS // run
            nc.gpsimd.memset(weights[:], 1.0 / BS)
            nc.gpsimd.affine_select(
                out=weights[:], in_=weights[:], compare_op=ALU.is_ge, fill=0.0,
                base=0, pattern=[[-span, P_BLOCKS * run]], channel_multiplier=1,
            )
            nc.gpsimd.affine_select(
                out=weights[:], in_=weights[:], compare_op=ALU.is_ge, fill=0.0,
                base=span - 1, pattern=[[span, P_BLOCKS * run]], channel_multiplier=-1,
            )
        nc.vector.memset(w_scales[:].bitcast(I32), 0)

        units = []
        for kv in range(HK):
            for head in [kv] + [HK + GROUP * kv + g for g in range(GROUP)]:
                for part in range(UNITS):
                    units.append((head, part))
        n_units = len(units)
        runs = [None] * SUMMED_UNITS + [2] * PAIRED_UNITS + [1] * (n_units - SUMMED_UNITS - PAIRED_UNITS)
        state = [{} for i in range(n_units)]
        heads = [k[0, kv] for kv in range(HK)] + [q[0, h] for h in range(HQ)]

        def load_unit(i):
            head, part = units[i]
            run = runs[i]
            positions = heads[head][UNIT_POSITIONS * part : UNIT_POSITIONS * (part + 1), :]
            if run is not None:
                by_position = loads.tile([P, UNIT_POSITIONS // P, D], BF16)
                nc.sync.dma_start(
                    out=by_position[:].rearrange("p (n e) d -> p n (e d)", e=run),
                    in_=positions.rearrange("(n p e) d -> p n (e d)", p=P, e=run),
                )
                state[i]["by_position"] = by_position
            by_block = loads.tile([P, UNIT_TILES, BS * D], BF16)
            rows = positions.rearrange("(c p j) d -> p c (j d)", c=UNIT_TILES, p=P)
            for some in WHOLE if run is not None else TILE_BY_TILE:
                nc.sync.dma_start(out=by_block[:, some, :], in_=rows[:, some, :])
            state[i]["by_block"] = by_block
            if part == 0:
                words = wk_words[head] if head < HK else wq_words[head - HK]
                nc.sync.dma_start(out=w_words[:, head, :], in_=words.rearrange("p n t -> p (n t)").bitcast(I32))

        def load_scales(first, count, scales):
            some = slice(first, first + count)
            for quad in range(4):
                nc.sync.dma_start(
                    out=w_scales[32 * quad : 32 * quad + 4, some, :].bitcast(I32),
                    in_=scales[:, 4 * quad : 4 * quad + 4, :].rearrange("g r n -> r g n").bitcast(I32),
                )

        def load_rope_tables():
            cos_rows = cos[0].rearrange("(c p) h -> p c h", p=P)
            sin_rows = sin[0].rearrange("(c p) h -> p c h", p=P)
            nc.sync.dma_start(out=rope[:, :, 0, :], in_=cos_rows)
            nc.sync.dma_start(out=rope[:, :, 1, 0:HALF], in_=sin_rows[:, :, HALF:])
            nc.sync.dma_start(out=rope[:, :, 1, HALF:], in_=sin_rows[:, :, 0:HALF])

        def negate_rope_half():
            nc.vector.tensor_scalar_mul(rope[:, :, 1, HALF:], rope[:, :, 1, HALF:], -1.0)

        def load_mask(part):
            some = slice(UNIT_TILES * part, UNIT_TILES * (part + 1))
            nc.sync.dma_start(
                out=mask_words[:, some, :],
                in_=attention_mask.bitcast(I32)[0, 0].rearrange("(c p) w -> p c w", p=P)[:, some, :],
            )

        def make_mask_bias(part):
            some = slice(UNIT_TILES * part, UNIT_TILES * (part + 1))
            nc.scalar.activation(
                out=mask_bias[:, some, :],
                in_=mask_words[:, some, :].bitcast(U32).rearrange("p c (j w) -> p c j w", w=2)[:, :, :, 0],
                func=ACT.Copy,
                scale=MASKED,
                bias=-MASKED,
            )

        def sum_positions(i):
            s, run = state[i], runs[i]
            mean_t = flip_psum.tile([P, 2, UNIT_BLOCKS], F32)
            width = P_BLOCKS * run
            for n in range(UNIT_BLOCKS // width):
                for f in range(2):
                    for e in range(run):
                        nc.tensor.matmul(
                            out=mean_t[:, f, width * n : width * (n + 1)],
                            lhsT=s["by_position"][:, run * n + e, P * f : P * (f + 1)],
                            rhs=block_mean[run][:],
                            start=e == 0,
                            stop=e == run - 1,
                        )
            s["mean_t"] = mean_t

        def pair_positions(i):
            for c in range(UNIT_TILES):
                by_block = state[i]["by_block"]
                pairs = sums_pool.tile([P, BS // 2, D], F32, tag=f"pairs_{c}")
                nc.vector.tensor_tensor(
                    out=pairs[:].rearrange("p j d -> p (j d)"),
                    in0=by_block[:, c, 0 : 4 * D], in1=by_block[:, c, 4 * D :], op=ALU.add,
                )
                state[i]["pairs", c] = pairs

        def sum_pairs(i):
            mean_t = flip_psum.tile([P, 2, UNIT_BLOCKS], F32)
            for c in range(UNIT_TILES):
                for f in range(2):
                    for j in range(BS // 2):
                        nc.tensor.matmul(
                            out=mean_t[:, f, P * c : P * (c + 1)],
                            lhsT=state[i]["pairs", c][:, j, P * f : P * (f + 1)],
                            rhs=ident[:],
                            is_transpose=True, start=j == 0, stop=j == BS // 2 - 1,
                        )
            state[i]["mean_t"] = mean_t

        def round_means(i):
            mean_bf = work.tile([P, 2, UNIT_BLOCKS], BF16)
            if runs[i] is None:
                nc.scalar.activation(out=mean_bf[:], in_=state[i]["mean_t"][:], func=ACT.Copy, scale=1.0 / BS)
            else:
                nc.scalar.copy(out=mean_bf[:], in_=state[i]["mean_t"][:])
            state[i]["mean_bf"] = mean_bf

        def flip_means(i):
            mean_rows = flip_psum.tile([P, UNIT_TILES, D], BF16)
            for c in range(UNIT_TILES):
                for f in range(2):
                    nc.tensor.transpose(
                        mean_rows[:, c, P * f : P * (f + 1)],
                        state[i]["mean_bf"][:, f, P * c : P * (c + 1)],
                        ident_bf[:],
                    )
            state[i]["mean_rows"] = mean_rows

        def new_pooled(i):
            pooled = work.tile([P, UNIT_TILES, K], BF16)
            state[i]["pooled"] = pooled

        def place_means(i):
            nc.scalar.copy(out=state[i]["pooled"][:, :, 0:D], in_=state[i]["mean_rows"][:])

        def max_of_8(i):
            max4 = work.tile([P, UNIT_TILES, 4 * D], BF16)
            by_block = state[i]["by_block"]
            for some in WHOLE if runs[i] is not None else TILE_BY_TILE:
                nc.vector.tensor_tensor(
                    out=max4[:, some, :], in0=by_block[:, some, 0 : 4 * D], in1=by_block[:, some, 4 * D :], op=ALU.max
                )
            state[i]["max4"] = max4

        def max_of_4(i):
            max2 = work.tile([P, UNIT_TILES, 2 * D], BF16)
            max4 = state[i]["max4"]
            nc.vector.tensor_tensor(out=max2[:], in0=max4[:, :, 0 : 2 * D], in1=max4[:, :, 2 * D :], op=ALU.max)
            state[i]["max2"] = max2

        def max_of_2(i):
            max2 = state[i]["max2"]
            nc.vector.tensor_tensor(
                out=state[i]["pooled"][:, :, D:], in0=max2[:, :, 0:D], in1=max2[:, :, D:], op=ALU.max
            )

        def flip_pooled(i):
            flipped = flip_psum.tile([P, UNIT_TILES, 2, P], F32)
            for c in range(UNIT_TILES):
                words = state[i]["pooled"][:, c, :].bitcast(F32)
                for u in range(2):
                    nc.tensor.transpose(flipped[:, c, u, :], words[:, u : K // 2 : 2], ident[:])
            state[i]["flipped"] = flipped

        def group_pooled(i):
            p_grouped = work.tile([P, UNIT_BLOCKS * PACK], BF16, align_bytes=64)
            nc.scalar.copy(
                out=p_grouped[:].bitcast(F32).rearrange("p (c b u) -> p c b u", c=UNIT_TILES, u=2),
                in_=state[i]["flipped"][:].rearrange("p c u b -> p c b u"),
            )
            state[i]["p_grouped"] = p_grouped

        def quantise_pooled(i):
            p_codes = work.tile([P, UNIT_BLOCKS], U32, align_bytes=64)
            p_scales = work.tile([P, UNIT_BLOCKS], U8, align_bytes=64)
            nc.vector.quantize_mx(out=p_codes[:].bitcast(FP8X4), scales=p_scales[:], in_=state[i]["p_grouped"][:])
            state[i]["p_codes"], state[i]["p_scales"] = p_codes, p_scales

        def project(i, c):
            head = units[i][0]
            blocks = slice(P * c, P * (c + 1))
            proj = mx_psum.tile([P, HID], F32)
            nc.tensor.matmul_mx(
                out=proj[:],
                lhsT=state[i]["p_codes"][:, blocks].bitcast(FP8X4),
                lhsT_scale=state[i]["p_scales"][:, blocks],
                rhs=w_words[:, head, :].bitcast(FP8X4),
                rhs_scale=w_scales[:, head, :],
                start=True,
                stop=True,
            )
            state[i]["proj", c] = proj

        def rotate(i, c):
            products = work.tile([P, 2, HID], F32)
            nc.vector.tensor_tensor(
                out=products[:],
                in0=state[i]["proj", c][:].unsqueeze(1).to_broadcast([P, 2, HID]),
                in1=rope[:, UNIT_TILES * units[i][1] + c, :, :],
                op=ALU.mult,
            )
            state[i]["products", c] = products

        def flip_rotated(i, c):
            products = state[i]["products", c]
            rotated_t = flip_psum.tile([P, PACK, P], F32)
            for t in range(PACK):
                swapped = (P * t + HALF) % HID
                nc.tensor.matmul(
                    out=rotated_t[:, t, :], lhsT=products[:, 0, P * t : P * (t + 1)], rhs=ident[:],
                    is_transpose=True, start=True, stop=False,
                )
                nc.tensor.matmul(
                    out=rotated_t[:, t, :], lhsT=products[:, 1, swapped : swapped + P], rhs=ident[:],
                    is_transpose=True, start=False, stop=True,
                )
            state[i]["rotated_t"] = rotated_t

        def group_rotated(i, c):
            if c == 0:
                r_grouped = work.tile([P, UNIT_BLOCKS, PACK], BF16, align_bytes=64)
                state[i]["r_grouped"] = r_grouped
            nc.scalar.copy(
                out=state[i]["r_grouped"][:, P * c : P * (c + 1), :],
                in_=state[i]["rotated_t"][:].rearrange("p t b -> p b t"),
            )

        def new_codes(i):
            head, part = units[i]
            if head < HK:
                some = slice(UNIT_BLOCKS * part, UNIT_BLOCKS * (part + 1))
                state[i]["codes"], state[i]["scales"] = k_codes[:, head, some], k_scales[:, head, some]
            else:
                q_codes = work.tile([P, UNIT_BLOCKS], U32, align_bytes=64)
                q_scales = work.tile([P, UNIT_BLOCKS], U8, align_bytes=64)
                state[i]["codes"], state[i]["scales"] = q_codes[:], q_scales[:]

        def quantise_rotated(i, some):
            blocks = slice(P * some.start, P * some.stop)
            nc.vector.quantize_mx(
                out=state[i]["codes"][:, blocks].bitcast(FP8X4),
                scales=state[i]["scales"][:, blocks],
                in_=state[i]["r_grouped"][:, blocks, :].rearrange("p b t -> p (b t)"),
            )

        def score(i, some):
            kv = (units[i][0] - HK) // GROUP
            for c in range(some.start, some.stop):
                blocks = slice(P * c, P * (c + 1))
                scores = mx_psum.tile([P, NB], F32)
                nc.tensor.matmul_mx(
                    out=scores[:],
                    lhsT=state[i]["codes"][:, blocks].bitcast(FP8X4),
                    lhsT_scale=state[i]["scales"][:, blocks],
                    rhs=k_codes[:, kv, :].bitcast(FP8X4),
                    rhs_scale=k_scales[:, kv, :],
                    start=True,
                    stop=True,
                )
                state[i]["scores", c] = scores

        def mask_scores(i, c):
            masked = work.tile([P, NB], F32, tag=f"masked_{c}")
            state[i]["masked", c] = masked
            nc.vector.scalar_tensor_tensor(
                out=masked[:],
                in0=state[i]["scores", c][:],
                scalar=1.0 / math.sqrt(HID),
                in1=mask_bias[:, UNIT_TILES * units[i][1] + c, :],
                op0=ALU.mult,
                op1=ALU.add,
            )

        def row_max(i, c):
            neg_max = stats_pool.tile([P, 1], F32)
            nc.vector.tensor_reduce(
                out=neg_max[:], in_=state[i]["masked", c][:], axis=AXIS.X, op=ALU.max, negate=True
            )
            state[i]["neg_max", c] = neg_max

        def exponentials(i):
            probs = probs_pool.tile([P, UNIT_TILES, NB], F32)
            total = stats_pool.tile([P, UNIT_TILES], F32)
            for c in range(UNIT_TILES):
                nc.scalar.activation(
                    out=probs[:, c, :], in_=state[i]["masked", c][:], func=ACT.Exp,
                    bias=state[i]["neg_max", c][:], scale=1.0, accum_out=total[:, c : c + 1],
                )
            state[i]["probs"], state[i]["total"] = probs, total

        def invert(i):
            inverse = stats_pool.tile([P, UNIT_TILES], F32)
            nc.vector.reciprocal(inverse[:], state[i]["total"][:])
            state[i]["inverse"] = inverse

        def normalise(i, c):
            rows = state[i]["probs"][:, c, :]
            nc.scalar.activation(out=rows, in_=rows, func=ACT.Copy, scale=state[i]["inverse"][:, c : c + 1])

        def normalise_on_vector(i, c):
            rows = state[i]["probs"][:, c, :]
            nc.vector.tensor_scalar_mul(rows, rows, state[i]["inverse"][:, c : c + 1])

        def store(i):
            head, part = units[i]
            rows = out[0, head - HK, UNIT_BLOCKS * part : UNIT_BLOCKS * (part + 1), :]
            for some in TILE_BY_TILE if i == n_units - 1 else WHOLE:
                nc.sync.dma_start(
                    out=rows.rearrange("(c p) j -> p c j", p=P)[:, some, :], in_=state[i]["probs"][:, some, :]
                )

        def unit_at(i):
            return 0 <= i < n_units

        def query_at(i):
            return 0 <= i < n_units and units[i][0] >= HK

        ctx.enter_context(tc.manual_schedule())
        load_unit(0)
        load_scales(0, HK, wk_scales)
        load_unit(1)
        load_rope_tables()
        load_unit(2)
        load_scales(HK, HQ, wq_scales)
        for i in range(n_units + 4 + STORE_LAG):
            new, old, turn, last, end = unit_at(i), unit_at(i - 1), unit_at(i - 2), unit_at(i - 3), query_at(i - 4)
            attend = query_at(i - 3)
            drain = i >= n_units + 2
            if unit_at(i + LOADS_AHEAD):
                load_unit(i + LOADS_AHEAD)
            if i in (0, 2):
                load_mask(i // 2)
            if query_at(i - 4 - STORE_LAG):
                store(i - 4 - STORE_LAG)
            if end:
                exponentials(i - 4)
            if turn:
                rotate(i - 2, 0)
            if last and not drain:
                new_codes(i - 3)
                quantise_rotated(i - 3, WHOLE[0])
            if turn:
                flip_rotated(i - 2, 0)
            if attend and not drain:
                score(i - 3, WHOLE[0])
            if turn:
                group_rotated(i - 2, 0)
            if new:
                if runs[i] is None:
                    pair_positions(i)
                new_pooled(i)
                max_of_8(i)
                if runs[i] is None:
                    sum_pairs(i)
                else:
                    sum_positions(i)
            if turn:
                rotate(i - 2, 1)
            if end and not drain:
                invert(i - 4)
                for c in range(UNIT_TILES):
                    normalise(i - 4, c)
            if old:
                quantise_pooled(i - 1)
            if new:
                round_means(i)
                max_of_4(i)
            if turn:
                flip_rotated(i - 2, 1)
            if old:
                for c in range(UNIT_TILES):
                    project(i - 1, c)
            if turn:
                group_rotated(i - 2, 1)
            if attend and not drain:
                mask_scores(i - 3, 0)
            if new:
                max_of_2(i)
                flip_means(i)
                place_means(i)
            if attend and not drain:
                mask_scores(i - 3, 1)
            if i == 1:
                negate_rope_half()
            if i in (4, 5):
                make_mask_bias(i - 4)
            if new:
                flip_pooled(i)
                group_pooled(i)
            if i == n_units + 1:
                new_codes(i - 2)
                row_max(i - 3, 0)
                quantise_rotated(i - 2, TILE_BY_TILE[0])
                score(i - 2, TILE_BY_TILE[0])
                row_max(i - 3, 1)
                mask_scores(i - 2, 0)
                quantise_rotated(i - 2, TILE_BY_TILE[1])
                score(i - 2, TILE_BY_TILE[1])
                row_max(i - 2, 0)
                mask_scores(i - 2, 1)
                row_max(i - 2, 1)
            elif attend and not drain:
                for c in range(UNIT_TILES):
                    row_max(i - 3, c)
            if end and drain:
                invert(i - 4)
                for c in range(UNIT_TILES):
                    if c == 0 and i - 4 == n_units - 1:
                        normalise(i - 4, c)
                    else:
                        normalise_on_vector(i - 4, c)
